import numpy as np
import ml_dtypes


def mxq(x, axis, fmt="e4m3"):
    dtype, down = {"e4m3": (ml_dtypes.float8_e4m3fn, 7), "e5m2": (ml_dtypes.float8_e5m2, 14)}[fmt]
    v = np.moveaxis(np.asarray(x, np.float32).astype(ml_dtypes.bfloat16).astype(np.float64), axis, -1)
    blocks = v.reshape(v.shape[:-1] + (-1, 32))
    amax = np.abs(blocks).max(-1, keepdims=True)
    byte = np.maximum(np.where(amax > 0, np.frexp(amax)[1] - 1 + 127, 0) - down, 1)
    scale = np.exp2(byte - 127.0)
    codes = (blocks / scale).astype(np.float32).astype(dtype).astype(np.float64)
    return np.moveaxis((codes * scale).reshape(v.shape), -1, axis)


WIDE = False


def mx_kscale(k):
    if not WIDE:
        return np.ones(k)
    levels = np.array([10, -10, 5, -5, 0])
    if k % 512:
        return np.exp2(np.random.permutation(np.resize(levels, k // 32))).repeat(32)
    a = np.empty((k // 512, 16))
    for p in range(k // 512):
        a[p, :8] = np.random.permutation(np.resize(levels, 8))
        for g in range(8):
            far = levels[np.abs(levels - a[p, g]) >= 10]
            a[p, g + 8] = far[np.random.randint(len(far))]
    return np.exp2(a.ravel()).repeat(32)


BF16 = ml_dtypes.bfloat16


def bf(x):
    return np.asarray(x, np.float32).astype(BF16)


def f64(x):
    return np.asarray(x).astype(np.float64)


B, H, L, D, DV = 1, 2, 2048, 128, 256


def setup_inputs():
    keep = (np.random.random((B, L, L)) < 0.75) | np.eye(L, dtype=bool)
    s = mx_kscale(L)
    q = np.random.standard_normal((B, H, L, D)) * 1.2
    k = np.random.standard_normal((B, H, L, D)) * 1.2
    v = np.random.standard_normal((B, H, L, DV))
    pe_q = np.random.standard_normal((B, H, L, D)) * 1.2
    pe_k = np.random.standard_normal((B, H, L, D)) * 1.2
    pe_q[..., 0] = 1.0
    pe_k[..., 0] += np.log(s) * np.sqrt(D)
    v = v / s[:, None] * s.mean()
    return {"q": bf(q), "k": bf(k), "v": bf(v), "pe_q": bf(pe_q), "pe_k": bf(pe_k), "mask": bf(keep)}


def reference(q, k, v, pe_q, pe_k, mask):
    scale = D ** (-0.5)
    attn = (f64(q) @ f64(k).transpose(0, 1, 3, 2) + f64(pe_q) @ f64(pe_k).transpose(0, 1, 3, 2)) * scale
    attn = np.where(f64(mask)[:, None, :, :] != 0.0, attn, -np.inf)
    e = np.exp(attn - attn.max(-1, keepdims=True))
    return (mxq(e, 3, "e4m3") @ mxq(f64(v), 2, "e4m3")) / e.sum(-1, keepdims=True)

@@ -1,0 +1,315 @@
+from contextlib import ExitStack
+
+import concourse.mybir as mybir
+from concourse.masks import make_identity
+
+F32 = mybir.dt.float32
+BF16 = mybir.dt.bfloat16
+U32 = mybir.dt.uint32
+U8 = mybir.dt.uint8
+FP8X4 = mybir.dt.float8_e4m3fn_x4
+ALU = mybir.AluOpType
+ACT = mybir.ActivationFunctionType
+AX = mybir.AxisListType
+
+P = 128
+H = 2
+L = 2048
+D = 128
+DV = 256
+NT = L // P
+NU = H * NT
+CH = 512
+NCH = L // CH
+SCALE = D ** -0.5
+BIG = 1.0e30
+
+FLOPS = 2 * H * L * L * (2 * D + DV)
+
+
+def tile_attention_kernel(tc, q, k, v, pe_q, pe_k, mask, out):
+    nc = tc.nc
+    with ExitStack() as ctx:
+        keep = ctx.enter_context(tc.tile_pool(name="keep", bufs=1))
+        wpool = ctx.enter_context(tc.tile_pool(name="wpool", bufs=4))
+        epool = ctx.enter_context(tc.tile_pool(name="epool", bufs=3))
+        gpool = ctx.enter_context(tc.tile_pool(name="gpool", bufs=2))
+        cpool = ctx.enter_context(tc.tile_pool(name="cpool", bufs=2))
+        opool = ctx.enter_context(tc.tile_pool(name="opool", bufs=3))
+        small = ctx.enter_context(tc.tile_pool(name="small", bufs=6))
+        ps_s = ctx.enter_context(tc.psum_pool(name="ps_s", bufs=4))
+        ps_x = ctx.enter_context(tc.psum_pool(name="ps_x", bufs=2))
+        ps_o = ctx.enter_context(tc.psum_pool(name="ps_o", bufs=1))
+        ps_p = ctx.enter_context(tc.psum_pool(name="ps_p", bufs=1))
+
+        ident = keep.tile([P, P], BF16, name="ident")
+        make_identity(nc, ident[:])
+        negident = keep.tile([P, P], BF16, name="negident")
+        nc.vector.tensor_scalar_mul(out=negident[:], in0=ident[:], scalar1=-1.0)
+
+        raw = {}
+        for h in range(H):
+            for nm in ("q", "pq", "k", "pk"):
+                raw[(nm, h)] = keep.tile([P, NT, D], BF16, name="raw_%s%d" % (nm, h))
+        qq = [keep.tile([P, 2, NT, P], BF16, name="qq%d" % h) for h in range(H)]
+        kk = [keep.tile([P, 2, L], BF16, name="kk%d" % h) for h in range(H)]
+        mb = [keep.tile([P, L], BF16, name="mb%d" % i) for i in range(NT)]
+        vraw = [keep.tile([P, NCH, 4, DV], BF16, name="vraw%d" % h) for h in range(H)]
+        vcodes = [keep.tile([P, NCH * DV], U32, name="vcodes%d" % h, align_bytes=64) for h in range(H)]
+        vscl = [keep.tile([P, NCH * DV], U8, name="vscl%d" % h, align_bytes=64) for h in range(H)]
+
+        def load_keys(nm, src, h, lo, hi):
+            nc.sync.dma_start(
+                out=raw[(nm, h)][:, lo:hi, :],
+                in_=src[0, h].rearrange("(t p) d -> p t d", p=P)[:, lo:hi, :],
+            )
+
+        def load_queries(nm, src, h, lo, hi):
+            nc.sync.dma_start(
+                out=raw[(nm, h)][:, lo:hi, :],
+                in_=src[0, h].rearrange("(p t) d -> p t d", t=NT)[:, lo:hi, :],
+            )
+
+        def load_mask(i):
+            nc.sync.dma_start(out=mb[i][:], in_=mask[0].rearrange("(p t) c -> t p c", t=NT)[i])
+
+        def load_v(h):
+            nc.sync.dma_start(out=vraw[h][:], in_=v[0, h].rearrange("(g p t) n -> p g t n", p=P, t=4))
+
+        load_keys("k", k, 0, 0, 4)
+        load_keys("pk", pe_k, 0, 0, 4)
+        load_queries("q", q, 0, 0, 4)
+        load_queries("pq", pe_q, 0, 0, 4)
+        load_mask(0)
+        load_keys("k", k, 0, 4, 8)
+        load_keys("pk", pe_k, 0, 4, 8)
+        load_keys("k", k, 0, 8, NT)
+        load_keys("pk", pe_k, 0, 8, NT)
+        load_mask(1)
+        load_queries("q", q, 0, 4, NT)
+        load_queries("pq", pe_q, 0, 4, NT)
+        load_v(0)
+        load_mask(2)
+        load_mask(3)
+        load_keys("k", k, 1, 0, NT)
+        load_keys("pk", pe_k, 1, 0, NT)
+        load_mask(4)
+        load_queries("q", q, 1, 0, NT)
+        load_queries("pq", pe_q, 1, 0, NT)
+        load_mask(5)
+        load_v(1)
+        for i in range(6, NT):
+            load_mask(i)
+
+        warm = small.tile([P, 1], F32, tag="warm", name="warm", bufs=1)
+        nc.vector.memset(warm[:], 0.0)
+        nc.scalar.activation(out=warm[:], in_=warm[:], func=ACT.Exp)
+
+        def bias_from_mask(eng, i, lo, hi):
+            eng.tensor_scalar(
+                out=mb[i][:, lo:hi], in0=mb[i][:, lo:hi],
+                scalar1=-1.0, scalar2=-BIG, op0=ALU.add, op1=ALU.mult,
+            )
+
+        vg = {}
+
+        def regroup_v(h):
+            vg[h] = gpool.tile([P, NCH, DV, 4], BF16, tag="vg", name="vg", bufs=1, align_bytes=64)
+            for g in range(NCH):
+                nc.gpsimd.tensor_scalar(
+                    out=vg[h][:, g, :, :],
+                    in0=vraw[h][:, g, :, :].rearrange("p t n -> p n t"),
+                    scalar1=1.0, scalar2=0.0, op0=ALU.mult, op1=ALU.add,
+                )
+
+        def quantise_v(h):
+            nc.vector.quantize_mx(
+                out=vcodes[h][:].bitcast(FP8X4),
+                scales=vscl[h][:],
+                in_=vg[h][:].rearrange("p g n t -> p (g n t)"),
+            )
+
+        def flip(pool, tag, a, b, h, c, dst, copy):
+            bank = pool.tile([P, 8, P], BF16, tag=tag, name="flip")
+            for n in range(8):
+                src = raw[(a if n < 4 else b, h)]
+                nc.tensor.transpose(bank[:, n, :], src[:, 4 * c + n % 4, :], ident[:])
+            copy(out=dst, in_=bank[:].rearrange("p (x c) r -> p x (c r)", x=2))
+
+        def flip_keys(pool, tag, h, c, copy):
+            flip(pool, tag, "k", "pk", h, c, kk[h][:, :, CH * c:CH * (c + 1)], copy)
+
+        def flip_queries(pool, tag, h, c, copy):
+            dst = qq[h][:, :, 4 * c:4 * c + 4, :].rearrange("p x c r -> p x (c r)")
+            flip(pool, tag, "q", "pq", h, c, dst, copy)
+
+        st = {}
+
+        def pe_masked(u):
+            return u % 4 != 3
+
+        def scores(u):
+            h, i = divmod(u, NT)
+            banks = []
+            for j in range(NCH):
+                s = ps_s.tile([P, CH], F32, tag="s", name="s")
+                cols = slice(CH * j, CH * (j + 1))
+                nc.tensor.matmul(s[:], lhsT=qq[h][:, 0, i, :], rhs=kk[h][:, 0, cols], start=True, stop=False)
+                extra = j == NCH - 1 and pe_masked(u)
+                nc.tensor.matmul(s[:], lhsT=qq[h][:, 1, i, :], rhs=kk[h][:, 1, cols], start=False, stop=not extra)
+                if extra:
+                    nc.tensor.matmul(s[:], lhsT=negident[:], rhs=mb[i][:, cols], start=False, stop=True)
+                banks.append(s)
+            st[("s", u)] = banks
+
+        def mask_and_min(u):
+            i = u % NT
+            w = wpool.tile([P, L], F32, tag="w", name="w")
+            nv = NCH - 1 if pe_masked(u) else NCH
+            for j in range(nv):
+                cols = slice(CH * j, CH * (j + 1))
+                nc.vector.scalar_tensor_tensor(
+                    out=w[:, cols], in0=st[("s", u)][j][:], scalar=-SCALE, in1=mb[i][:, cols],
+                    op0=ALU.mult, op1=ALU.add,
+                )
+            wmin = small.tile([P, 1], F32, tag="wmin", name="wmin")
+            if pe_masked(u):
+                vmin = small.tile([P, 1], F32, tag="vmin", name="vmin")
+                nc.vector.tensor_reduce(out=vmin[:], in_=w[:, 0:CH * nv], axis=AX.X, op=ALU.min)
+                nc.vector.tensor_scalar(
+                    out=w[:, CH * nv:L], in0=st[("s", u)][nv][:], scalar1=-SCALE, scalar2=vmin[:],
+                    op0=ALU.mult, op1=ALU.min, accum_out=wmin[:],
+                )
+            else:
+                nc.vector.tensor_reduce(out=wmin[:], in_=w[:], axis=AX.X, op=ALU.min)
+            st[("w", u)] = w
+            st[("wmin", u)] = wmin
+
+        def pieces(u):
+            return 2 if u == NU - 1 else 1
+
+        def exponent(u):
+            e = epool.tile([P, L], BF16, tag="e", name="e")
+            width = L // pieces(u)
+            sums = []
+            for a in range(pieces(u)):
+                rs = small.tile([P, 1], F32, tag="rs", name="rs")
+                cols = slice(a * width, (a + 1) * width)
+                nc.scalar.activation(
+                    out=e[:, cols], in_=st[("w", u)][:, cols], func=ACT.Exp, bias=st[("wmin", u)][:], scale=-1.0,
+                    accum_out=rs[:],
+                )
+                sums.append(rs)
+            st[("e", u)] = e
+            st[("rs", u)] = sums
+
+        def flip_e(u):
+            e = st[("e", u)]
+            banks = []
+            for b in range(2):
+                xt = ps_x.tile([P, 8, P], BF16, tag="xt", name="xt")
+                for n in range(8):
+                    g, t = divmod(8 * b + n, 4)
+                    nc.tensor.transpose(xt[:, n, :], e[:, CH * g + t:CH * (g + 1):4], ident[:])
+                banks.append(xt)
+            st[("xt", u)] = banks
+
+        def group_e(u):
+            gr = gpool.tile([P, NCH, P, 4], BF16, tag="gr", name="gr", align_bytes=64)
+            for b in range(2):
+                copy = nc.vector.tensor_copy if (u >= NU - 2 and b == 0) else nc.scalar.copy
+                copy(
+                    out=gr[:, 2 * b:2 * b + 2, :, :],
+                    in_=st[("xt", u)][b][:].rearrange("p (g t) r -> p g r t", t=4),
+                )
+            st[("gr", u)] = gr
+
+        def quantise_e(u):
+            codes = cpool.tile([P, NCH * P], U32, tag="codes", name="codes", align_bytes=64)
+            scl = cpool.tile([P, NCH * P], U8, tag="scl", name="scl", align_bytes=64)
+            n = pieces(u)
+            for a in range(n):
+                words = slice(a * NCH * P // n, (a + 1) * NCH * P // n)
+                nc.vector.quantize_mx(
+                    out=codes[:, words].bitcast(FP8X4), scales=scl[:, words],
+                    in_=st[("gr", u)][:, a * NCH // n:(a + 1) * NCH // n, :, :].rearrange("p g r t -> p (g r t)"),
+                )
+            rinv = small.tile([P, 1], F32, tag="rinv", name="rinv")
+            sums = st[("rs", u)]
+            if n == 2:
+                nc.vector.tensor_tensor(out=sums[0][:], in0=sums[0][:], in1=sums[1][:], op=ALU.add)
+            nc.vector.reciprocal(rinv[:], sums[0][:])
+            st[("codes", u)] = codes
+            st[("scl", u)] = scl
+            st[("rinv", u)] = rinv
+
+        def weighted_sum(u):
+            h, i = divmod(u, NT)
+            o = ps_o.tile([P, DV], F32, tag="o", name="o")
+            for g in range(NCH):
+                nc.tensor.matmul_mx(
+                    out=o[:],
+                    lhsT=st[("codes", u)][:, P * g:P * (g + 1)].bitcast(FP8X4),
+                    lhsT_scale=st[("scl", u)][:, P * g:P * (g + 1)],
+                    rhs=vcodes[h][:, DV * g:DV * (g + 1)].bitcast(FP8X4),
+                    rhs_scale=vscl[h][:, DV * g:DV * (g + 1)],
+                    start=(g == 0), stop=(g == NCH - 1),
+                )
+            res = opool.tile([P, DV], F32, tag="res", name="res")
+            if u >= NU - 3:
+                nc.vector.tensor_scalar_mul(out=res[:], in0=o[:], scalar1=st[("rinv", u)][:])
+            else:
+                nc.scalar.activation(out=res[:], in_=o[:], func=ACT.Copy, scale=st[("rinv", u)][:])
+            nc.sync.dma_start(out=out[0, h].rearrange("(p t) n -> t p n", t=NT)[i], in_=res[:])
+
+        vcopy = nc.vector.tensor_copy
+        scopy = nc.scalar.copy
+        flip_queries(ps_x, "xt", 0, 0, vcopy)
+        flip_keys(ps_s, "s", 0, 0, scopy)
+        for j in range(NCH):
+            bias_from_mask(nc.vector, 0, CH * j, CH * (j + 1))
+        flip_keys(ps_s, "s", 0, 1, vcopy)
+        flip_keys(ps_s, "s", 0, 2, scopy)
+        flip_keys(ps_s, "s", 0, 3, vcopy)
+        scores(0)
+        for c in range(1, 4):
+            flip_queries(ps_p, "p", 0, c, scopy)
+
+        bias_from_mask(nc.gpsimd, 1, 0, L)
+        regroup_v(0)
+        for i in range(2, 7):
+            bias_from_mask(nc.gpsimd, i, 0, L)
+
+        later = {}
+        for c in range(4):
+            later[3 + c] = ("k", c)
+            later[7 + c] = ("q", c)
+
+        for s in range(NU + 2):
+            if s < NU:
+                mask_and_min(s)
+            if s + 1 < NU:
+                scores(s + 1)
+            if 1 <= s <= NU:
+                flip_e(s - 1)
+            if s < NU:
+                exponent(s)
+            if 1 <= s <= NU:
+                group_e(s - 1)
+            if s == 1:
+                quantise_v(0)
+            if s == 2:
+                regroup_v(1)
+                for i in range(7, NT):
+                    bias_from_mask(nc.gpsimd, i, 0, L)
+            if s == 12:
+                quantise_v(1)
+            if s >= 2:
+                quantise_e(s - 2)
+                weighted_sum(s - 2)
+            if s in later:
+                kind, c = later[s]
+                if kind == "k":
+                    flip_keys(ps_p, "p", 1, c, scopy if c % 2 else vcopy)
+                else:
+                    flip_queries(ps_p, "p", 1, c, scopy if c % 2 else vcopy)

@@ -21,8 +21,11 @@ NT = L // P
 NU = H * NT
 CH = 512
 NCH = L // CH
+HALF = L // 2
+ORDER = (0, 1, 2, 3)
 SCALE = D ** -0.5
 BIG = 1.0e30
+PAD = 8
 
 FLOPS = 2 * H * L * L * (2 * D + DV)
 
@@ -31,37 +34,42 @@ def tile_attention_kernel(tc, q, k, v, pe_q, pe_k, mask, out):
     nc = tc.nc
     with ExitStack() as ctx:
         keep = ctx.enter_context(tc.tile_pool(name="keep", bufs=1))
+        mpool = ctx.enter_context(tc.tile_pool(name="mpool", bufs=3))
         wpool = ctx.enter_context(tc.tile_pool(name="wpool", bufs=4))
         epool = ctx.enter_context(tc.tile_pool(name="epool", bufs=3))
         gpool = ctx.enter_context(tc.tile_pool(name="gpool", bufs=2))
         cpool = ctx.enter_context(tc.tile_pool(name="cpool", bufs=2))
         opool = ctx.enter_context(tc.tile_pool(name="opool", bufs=3))
         small = ctx.enter_context(tc.tile_pool(name="small", bufs=6))
-        ps_s = ctx.enter_context(tc.psum_pool(name="ps_s", bufs=4))
+        ps_s = ctx.enter_context(tc.psum_pool(name="ps_s", bufs=5))
         ps_x = ctx.enter_context(tc.psum_pool(name="ps_x", bufs=2))
         ps_o = ctx.enter_context(tc.psum_pool(name="ps_o", bufs=1))
-        ps_p = ctx.enter_context(tc.psum_pool(name="ps_p", bufs=1))
 
         ident = keep.tile([P, P], BF16, name="ident")
         make_identity(nc, ident[:])
+        ident32 = keep.tile([P, P], F32, name="ident32")
+        make_identity(nc, ident32[:])
         negident = keep.tile([P, P], BF16, name="negident")
         nc.vector.tensor_scalar_mul(out=negident[:], in0=ident[:], scalar1=-1.0)
 
         raw = {}
-        for h in range(H):
-            for nm in ("q", "pq", "k", "pk"):
-                raw[(nm, h)] = keep.tile([P, NT, D], BF16, name="raw_%s%d" % (nm, h))
+
+        def make_raw(h):
+            for nm in ("q", "pq"):
+                raw[(nm, h)] = keep.tile([P, NT, D], BF16, tag="raw_" + nm, name="raw_" + nm)
+            for nm in ("k", "pk"):
+                raw[(nm, h)] = keep.tile([P, NT // 2, 2, D], BF16, tag="raw_" + nm, name="raw_" + nm)
+
         qq = [keep.tile([P, 2, NT, P], BF16, name="qq%d" % h) for h in range(H)]
-        kk = [keep.tile([P, 2, L], BF16, name="kk%d" % h) for h in range(H)]
+        kk = [keep.tile([P, 2, 2, HALF], BF16, name="kk%d" % h) for h in range(H)]
         mb = [keep.tile([P, L], BF16, name="mb%d" % i) for i in range(NT)]
-        vraw = [keep.tile([P, NCH, 4, DV], BF16, name="vraw%d" % h) for h in range(H)]
         vcodes = [keep.tile([P, NCH * DV], U32, name="vcodes%d" % h, align_bytes=64) for h in range(H)]
         vscl = [keep.tile([P, NCH * DV], U8, name="vscl%d" % h, align_bytes=64) for h in range(H)]
 
         def load_keys(nm, src, h, lo, hi):
             nc.sync.dma_start(
-                out=raw[(nm, h)][:, lo:hi, :],
-                in_=src[0, h].rearrange("(t p) d -> p t d", p=P)[:, lo:hi, :],
+                out=raw[(nm, h)][:, lo:hi, :, :].rearrange("p m u d -> p m (u d)"),
+                in_=src[0, h].rearrange("(m p u) d -> p m (u d)", p=P, u=2)[:, lo:hi, :],
             )
 
         def load_queries(nm, src, h, lo, hi):
@@ -70,12 +78,22 @@ def tile_attention_kernel(tc, q, k, v, pe_q, pe_k, mask, out):
                 in_=src[0, h].rearrange("(p t) d -> p t d", t=NT)[:, lo:hi, :],
             )
 
+        mraw = {}
+
         def load_mask(i):
-            nc.sync.dma_start(out=mb[i][:], in_=mask[0].rearrange("(p t) c -> t p c", t=NT)[i])
+            mraw[i] = mpool.tile([P, L], BF16, tag="mraw", name="mraw")
+            nc.sync.dma_start(out=mraw[i][:], in_=mask[0].rearrange("(p t) c -> t p c", t=NT)[i])
+
+        vraw = {}
 
         def load_v(h):
-            nc.sync.dma_start(out=vraw[h][:], in_=v[0, h].rearrange("(g p t) n -> p g t n", p=P, t=4))
+            vraw[h] = gpool.tile([P, NCH, 4, DV], BF16, tag="vraw", name="vraw", bufs=1)
+            nc.sync.dma_start(
+                out=vraw[h][:].rearrange("p g t n -> p g (t n)"),
+                in_=v[0, h].rearrange("(g p t) n -> p g (t n)", p=P, t=4),
+            )
 
+        make_raw(0)
         load_keys("k", k, 0, 0, 4)
         load_keys("pk", pe_k, 0, 0, 4)
         load_queries("q", q, 0, 0, 4)
@@ -83,23 +101,11 @@ def tile_attention_kernel(tc, q, k, v, pe_q, pe_k, mask, out):
         load_mask(0)
         load_keys("k", k, 0, 4, 8)
         load_keys("pk", pe_k, 0, 4, 8)
-        load_keys("k", k, 0, 8, NT)
-        load_keys("pk", pe_k, 0, 8, NT)
         load_mask(1)
         load_queries("q", q, 0, 4, NT)
         load_queries("pq", pe_q, 0, 4, NT)
-        load_v(0)
         load_mask(2)
-        load_mask(3)
-        load_keys("k", k, 1, 0, NT)
-        load_keys("pk", pe_k, 1, 0, NT)
-        load_mask(4)
-        load_queries("q", q, 1, 0, NT)
-        load_queries("pq", pe_q, 1, 0, NT)
-        load_mask(5)
-        load_v(1)
-        for i in range(6, NT):
-            load_mask(i)
+        load_v(0)
 
         warm = small.tile([P, 1], F32, tag="warm", name="warm", bufs=1)
         nc.vector.memset(warm[:], 0.0)
@@ -107,138 +113,150 @@ def tile_attention_kernel(tc, q, k, v, pe_q, pe_k, mask, out):
 
         def bias_from_mask(eng, i, lo, hi):
             eng.tensor_scalar(
-                out=mb[i][:, lo:hi], in0=mb[i][:, lo:hi],
+                out=mb[i][:].rearrange("p (u n) -> p u n", u=2)[:, :, lo:hi],
+                in0=mraw[i][:].rearrange("p (n u) -> p u n", u=2)[:, :, lo:hi],
                 scalar1=-1.0, scalar2=-BIG, op0=ALU.add, op1=ALU.mult,
             )
 
         vg = {}
 
-        def regroup_v(h):
-            vg[h] = gpool.tile([P, NCH, DV, 4], BF16, tag="vg", name="vg", bufs=1, align_bytes=64)
-            for g in range(NCH):
-                nc.gpsimd.tensor_scalar(
-                    out=vg[h][:, g, :, :],
-                    in0=vraw[h][:, g, :, :].rearrange("p t n -> p n t"),
-                    scalar1=1.0, scalar2=0.0, op0=ALU.mult, op1=ALU.add,
-                )
+        def regroup_v(h, g):
+            if g == 0:
+                vg[h] = gpool.tile([P, NCH, DV, 2, 2], BF16, tag="vg", name="vg", bufs=1, align_bytes=64)
+            nc.gpsimd.tensor_scalar(
+                out=vg[h][:, g, :, :, :],
+                in0=vraw[h][:, g, :, :].rearrange("p (e u) n -> p n u e", u=2),
+                scalar1=1.0, scalar2=0.0, op0=ALU.mult, op1=ALU.add,
+            )
 
         def quantise_v(h):
             nc.vector.quantize_mx(
                 out=vcodes[h][:].bitcast(FP8X4),
                 scales=vscl[h][:],
-                in_=vg[h][:].rearrange("p g n t -> p (g n t)"),
+                in_=vg[h][:].rearrange("p g n u e -> p (g n u e)"),
             )
 
-        def flip(pool, tag, a, b, h, c, dst, copy):
-            bank = pool.tile([P, 8, P], BF16, tag=tag, name="flip")
-            for n in range(8):
-                src = raw[(a if n < 4 else b, h)]
-                nc.tensor.transpose(bank[:, n, :], src[:, 4 * c + n % 4, :], ident[:])
-            copy(out=dst, in_=bank[:].rearrange("p (x c) r -> p x (c r)", x=2))
+        def flip_keys(h, j, copy):
+            u, a = divmod(j, 2)
+            bank = ps_s.tile([P, 2, 4, P], BF16, tag="s", name="flip")
+            for x, nm in enumerate(("k", "pk")):
+                for m in range(4):
+                    nc.tensor.transpose(bank[:, x, m, :], raw[(nm, h)][:, 4 * a + m, u, :], ident[:])
+            copy(
+                out=kk[h][:, :, u, CH * a:CH * (a + 1)],
+                in_=bank[:].rearrange("p x m r -> p x (m r)"),
+            )
 
-        def flip_keys(pool, tag, h, c, copy):
-            flip(pool, tag, "k", "pk", h, c, kk[h][:, :, CH * c:CH * (c + 1)], copy)
-
-        def flip_queries(pool, tag, h, c, copy):
+        def flip_queries(h, c, copy):
+            bank = ps_s.tile([P, 2, 4, P], BF16, tag="s", name="flip")
+            for x, nm in enumerate(("q", "pq")):
+                for t in range(4):
+                    nc.tensor.transpose(bank[:, x, t, :], raw[(nm, h)][:, 4 * c + t, :], ident[:])
             dst = qq[h][:, :, 4 * c:4 * c + 4, :].rearrange("p x c r -> p x (c r)")
-            flip(pool, tag, "q", "pq", h, c, dst, copy)
+            copy(out=dst, in_=bank[:].rearrange("p x c r -> p x (c r)"))
 
         st = {}
 
-        def pe_masked(u):
-            return u % 4 != 3
+        def role(u, j):
+            if j == NCH - 1 and u % 4 != 3:
+                return "T"
+            if j == 0 and 3 <= u < NU - 2:
+                return "G"
+            return "V"
+
+        def keys(h, x, j):
+            n0 = CH * (j % 2)
+            return kk[h][:, x, j // 2, n0:n0 + CH]
 
         def scores(u):
             h, i = divmod(u, NT)
-            banks = []
-            for j in range(NCH):
+            for j in ORDER:
                 s = ps_s.tile([P, CH], F32, tag="s", name="s")
-                cols = slice(CH * j, CH * (j + 1))
-                nc.tensor.matmul(s[:], lhsT=qq[h][:, 0, i, :], rhs=kk[h][:, 0, cols], start=True, stop=False)
-                extra = j == NCH - 1 and pe_masked(u)
-                nc.tensor.matmul(s[:], lhsT=qq[h][:, 1, i, :], rhs=kk[h][:, 1, cols], start=False, stop=not extra)
+                nc.tensor.matmul(s[:], lhsT=qq[h][:, 0, i, :], rhs=keys(h, 0, j), start=True, stop=False)
+                extra = role(u, j) == "T"
+                nc.tensor.matmul(s[:], lhsT=qq[h][:, 1, i, :], rhs=keys(h, 1, j), start=False, stop=not extra)
                 if extra:
-                    nc.tensor.matmul(s[:], lhsT=negident[:], rhs=mb[i][:, cols], start=False, stop=True)
-                banks.append(s)
-            st[("s", u)] = banks
+                    nc.tensor.matmul(
+                        s[:], lhsT=negident[:], rhs=mb[i][:, CH * j:CH * (j + 1)], start=False, stop=True
+                    )
+                st[("s", u, j)] = s
 
-        def mask_and_min(u):
+        def w_columns(u, j):
+            return st[("w", u)][:, PAD + CH * j:PAD + CH * (j + 1)]
+
+        def leave_psum(u, who):
             i = u % NT
-            w = wpool.tile([P, L], F32, tag="w", name="w")
-            nv = NCH - 1 if pe_masked(u) else NCH
-            for j in range(nv):
-                cols = slice(CH * j, CH * (j + 1))
-                nc.vector.scalar_tensor_tensor(
-                    out=w[:, cols], in0=st[("s", u)][j][:], scalar=-SCALE, in1=mb[i][:, cols],
-                    op0=ALU.mult, op1=ALU.add,
-                )
-            wmin = small.tile([P, 1], F32, tag="wmin", name="wmin")
-            if pe_masked(u):
-                vmin = small.tile([P, 1], F32, tag="vmin", name="vmin")
-                nc.vector.tensor_reduce(out=vmin[:], in_=w[:, 0:CH * nv], axis=AX.X, op=ALU.min)
-                nc.vector.tensor_scalar(
-                    out=w[:, CH * nv:L], in0=st[("s", u)][nv][:], scalar1=-SCALE, scalar2=vmin[:],
-                    op0=ALU.mult, op1=ALU.min, accum_out=wmin[:],
-                )
-            else:
-                nc.vector.tensor_reduce(out=wmin[:], in_=w[:], axis=AX.X, op=ALU.min)
-            st[("w", u)] = w
-            st[("wmin", u)] = wmin
+            if ("w", u) not in st:
+                st[("w", u)] = wpool.tile([P, PAD + L], F32, tag="w", name="w")
+            for j in ORDER:
+                if role(u, j) not in who:
+                    continue
+                s = st[("s", u, j)]
+                bias = mb[i][:, CH * j:CH * (j + 1)]
+                dst = w_columns(u, j)
+                if role(u, j) == "T":
+                    nc.vector.tensor_scalar(
+                        out=dst, in0=s[:], scalar1=-SCALE, scalar2=None,
+                        op0=ALU.mult, op1=ALU.min, accum_out=st[("w", u)][:, PAD - 1:PAD],
+                    )
+                elif role(u, j) == "G":
+                    nc.scalar.activation(out=dst, in_=s[:], func=ACT.Copy, scale=-SCALE)
+                    nc.gpsimd.tensor_tensor(out=dst, in0=dst, in1=bias, op=ALU.add)
+                else:
+                    nc.vector.scalar_tensor_tensor(
+                        out=dst, in0=s[:], scalar=-SCALE, in1=bias, op0=ALU.mult, op1=ALU.add,
+                    )
 
-        def pieces(u):
-            return 2 if u == NU - 1 else 1
+        def find_min(u):
+            last = role(u, NCH - 1) == "T"
+            cols = slice(PAD - 1, PAD + CH * (NCH - 1)) if last else slice(PAD, PAD + L)
+            wmin = small.tile([P, 1], F32, tag="wmin", name="wmin")
+            nc.vector.tensor_reduce(out=wmin[:], in_=st[("w", u)][:, cols], axis=AX.X, op=ALU.min)
+            st[("wmin", u)] = wmin
 
         def exponent(u):
             e = epool.tile([P, L], BF16, tag="e", name="e")
-            width = L // pieces(u)
-            sums = []
-            for a in range(pieces(u)):
-                rs = small.tile([P, 1], F32, tag="rs", name="rs")
-                cols = slice(a * width, (a + 1) * width)
-                nc.scalar.activation(
-                    out=e[:, cols], in_=st[("w", u)][:, cols], func=ACT.Exp, bias=st[("wmin", u)][:], scale=-1.0,
-                    accum_out=rs[:],
-                )
-                sums.append(rs)
+            rs = small.tile([P, 1], F32, tag="rs", name="rs")
+            nc.scalar.activation(
+                out=e[:], in_=st[("w", u)][:, PAD:PAD + L], func=ACT.Exp, bias=st[("wmin", u)][:], scale=-1.0,
+                accum_out=rs[:],
+            )
             st[("e", u)] = e
-            st[("rs", u)] = sums
+            st[("rs", u)] = rs
 
         def flip_e(u):
-            e = st[("e", u)]
+            words = st[("e", u)][:].bitcast(F32)
             banks = []
             for b in range(2):
-                xt = ps_x.tile([P, 8, P], BF16, tag="xt", name="xt")
-                for n in range(8):
-                    g, t = divmod(8 * b + n, 4)
-                    nc.tensor.transpose(xt[:, n, :], e[:, CH * g + t:CH * (g + 1):4], ident[:])
+                xt = ps_x.tile([P, 2, 2, P], F32, tag="xt", name="xt")
+                for n in range(2):
+                    g = 2 * b + n
+                    for half in range(2):
+                        lo = CH * half + P * g
+                        nc.tensor.transpose(xt[:, n, half, :], words[:, lo:lo + P], ident32[:])
                 banks.append(xt)
             st[("xt", u)] = banks
 
         def group_e(u):
             gr = gpool.tile([P, NCH, P, 4], BF16, tag="gr", name="gr", align_bytes=64)
+            grw = gr[:].rearrange("p g r t -> p (g r t)").bitcast(F32).rearrange("p (g r u) -> p g r u", r=P, u=2)
             for b in range(2):
                 copy = nc.vector.tensor_copy if (u >= NU - 2 and b == 0) else nc.scalar.copy
                 copy(
-                    out=gr[:, 2 * b:2 * b + 2, :, :],
-                    in_=st[("xt", u)][b][:].rearrange("p (g t) r -> p g r t", t=4),
+                    out=grw[:, 2 * b:2 * b + 2, :, :],
+                    in_=st[("xt", u)][b][:].rearrange("p g u r -> p g r u"),
                 )
             st[("gr", u)] = gr
 
         def quantise_e(u):
             codes = cpool.tile([P, NCH * P], U32, tag="codes", name="codes", align_bytes=64)
             scl = cpool.tile([P, NCH * P], U8, tag="scl", name="scl", align_bytes=64)
-            n = pieces(u)
-            for a in range(n):
-                words = slice(a * NCH * P // n, (a + 1) * NCH * P // n)
-                nc.vector.quantize_mx(
-                    out=codes[:, words].bitcast(FP8X4), scales=scl[:, words],
-                    in_=st[("gr", u)][:, a * NCH // n:(a + 1) * NCH // n, :, :].rearrange("p g r t -> p (g r t)"),
-                )
+            nc.vector.quantize_mx(
+                out=codes[:].bitcast(FP8X4), scales=scl[:],
+                in_=st[("gr", u)][:].rearrange("p g r t -> p (g r t)"),
+            )
             rinv = small.tile([P, 1], F32, tag="rinv", name="rinv")
-            sums = st[("rs", u)]
-            if n == 2:
-                nc.vector.tensor_tensor(out=sums[0][:], in0=sums[0][:], in1=sums[1][:], op=ALU.add)
-            nc.vector.reciprocal(rinv[:], sums[0][:])
+            nc.vector.reciprocal(rinv[:], st[("rs", u)][:])
             st[("codes", u)] = codes
             st[("scl", u)] = scl
             st[("rinv", u)] = rinv
@@ -255,61 +273,83 @@ def tile_attention_kernel(tc, q, k, v, pe_q, pe_k, mask, out):
                     rhs_scale=vscl[h][:, DV * g:DV * (g + 1)],
                     start=(g == 0), stop=(g == NCH - 1),
                 )
+            st[("o", u)] = o
+
+        def finish(u):
+            h, i = divmod(u, NT)
+            o = st[("o", u)]
             res = opool.tile([P, DV], F32, tag="res", name="res")
-            if u >= NU - 3:
-                nc.vector.tensor_scalar_mul(out=res[:], in0=o[:], scalar1=st[("rinv", u)][:])
-            else:
-                nc.scalar.activation(out=res[:], in_=o[:], func=ACT.Copy, scale=st[("rinv", u)][:])
+            nc.scalar.activation(out=res[:], in_=o[:], func=ACT.Copy, scale=st[("rinv", u)][:])
             nc.sync.dma_start(out=out[0, h].rearrange("(p t) n -> t p n", t=NT)[i], in_=res[:])
 
         vcopy = nc.vector.tensor_copy
         scopy = nc.scalar.copy
-        flip_queries(ps_x, "xt", 0, 0, vcopy)
-        flip_keys(ps_s, "s", 0, 0, scopy)
-        for j in range(NCH):
-            bias_from_mask(nc.vector, 0, CH * j, CH * (j + 1))
-        flip_keys(ps_s, "s", 0, 1, vcopy)
-        flip_keys(ps_s, "s", 0, 2, scopy)
-        flip_keys(ps_s, "s", 0, 3, vcopy)
+        flip_keys(0, 0, vcopy)
+        flip_queries(0, 0, scopy)
+        flip_keys(0, 2, scopy)
+        for half in range(2):
+            bias_from_mask(nc.vector, 0, CH * half, CH * (half + 1))
+        flip_keys(0, 1, vcopy)
+        flip_keys(0, 3, scopy)
+        bias_from_mask(nc.gpsimd, 1, 0, HALF)
+        bias_from_mask(nc.gpsimd, 2, 0, HALF)
+        load_mask(3)
         scores(0)
         for c in range(1, 4):
-            flip_queries(ps_p, "p", 0, c, scopy)
-
-        bias_from_mask(nc.gpsimd, 1, 0, L)
-        regroup_v(0)
-        for i in range(2, 7):
-            bias_from_mask(nc.gpsimd, i, 0, L)
+            flip_queries(0, c, scopy)
+        make_raw(1)
+        load_keys("k", k, 1, 0, 8)
+        load_keys("pk", pe_k, 1, 0, 8)
 
         later = {}
         for c in range(4):
             later[3 + c] = ("k", c)
             later[7 + c] = ("q", c)
 
-        for s in range(NU + 2):
-            if s < NU:
-                mask_and_min(s)
-            if s + 1 < NU:
-                scores(s + 1)
-            if 1 <= s <= NU:
-                flip_e(s - 1)
-            if s < NU:
-                exponent(s)
-            if 1 <= s <= NU:
-                group_e(s - 1)
-            if s == 1:
-                quantise_v(0)
-            if s == 2:
-                regroup_v(1)
-                for i in range(7, NT):
-                    bias_from_mask(nc.gpsimd, i, 0, L)
-            if s == 12:
-                quantise_v(1)
-            if s >= 2:
-                quantise_e(s - 2)
-                weighted_sum(s - 2)
-            if s in later:
-                kind, c = later[s]
-                if kind == "k":
-                    flip_keys(ps_p, "p", 1, c, scopy if c % 2 else vcopy)
+        with tc.manual_schedule():
+            for s in range(NU + 3):
+                if s < NU:
+                    leave_psum(s, "VTG")
+                if s >= 3 and s - 3 < NU:
+                    quantise_e(s - 3)
+                if s == 3:
+                    quantise_v(0)
+                if s == 18:
+                    quantise_v(1)
+                if s < NU:
+                    find_min(s)
+                if 2 <= s <= NU + 1:
+                    flip_e(s - 2)
+                if s + 1 < NU:
+                    scores(s + 1)
+                if s >= 4:
+                    finish(s - 4)
+                if 1 <= s <= NU:
+                    exponent(s - 1)
+                if 2 <= s <= NU + 1:
+                    group_e(s - 2)
+                if s >= 3 and s - 3 < NU:
+                    weighted_sum(s - 3)
+                if s + 4 < NT:
+                    load_mask(s + 4)
+                if s == 1:
+                    for g in range(NCH):
+                        regroup_v(0, g)
                 else:
-                    flip_queries(ps_p, "p", 1, c, scopy if c % 2 else vcopy)
+                    i = s + 3 if s == 0 else s + 2
+                    if i < NT:
+                        bias_from_mask(nc.gpsimd, i, 0, HALF)
+                if s == 1:
+                    load_queries("q", q, 1, 0, NT)
+                    load_queries("pq", pe_q, 1, 0, NT)
+                if s == 3:
+                    load_v(1)
+                if 14 <= s < 18:
+                    regroup_v(1, s - 14)
+                if s in later:
+                    kind, c = later[s]
+                    if kind == "k":
+                        flip_keys(1, c, scopy)
+                    else:
+                        flip_queries(1, c, scopy)
+            finish(NU - 1)

@@ -25,6 +25,7 @@ HALF = L // 2
 ORDER = (0, 1, 2, 3)
 SCALE = D ** -0.5
 BIG = 1.0e30
+FIRST_G = 6
 PAD = 8
 
 FLOPS = 2 * H * L * L * (2 * D + DV)
@@ -38,7 +39,7 @@ def tile_attention_kernel(tc, q, k, v, pe_q, pe_k, mask, out):
         wpool = ctx.enter_context(tc.tile_pool(name="wpool", bufs=4))
         epool = ctx.enter_context(tc.tile_pool(name="epool", bufs=3))
         gpool = ctx.enter_context(tc.tile_pool(name="gpool", bufs=2))
-        cpool = ctx.enter_context(tc.tile_pool(name="cpool", bufs=2))
+        cpool = ctx.enter_context(tc.tile_pool(name="cpool", bufs=3))
         opool = ctx.enter_context(tc.tile_pool(name="opool", bufs=3))
         small = ctx.enter_context(tc.tile_pool(name="small", bufs=6))
         ps_s = ctx.enter_context(tc.psum_pool(name="ps_s", bufs=5))
@@ -53,13 +54,11 @@ def tile_attention_kernel(tc, q, k, v, pe_q, pe_k, mask, out):
         nc.vector.tensor_scalar_mul(out=negident[:], in0=ident[:], scalar1=-1.0)
 
         raw = {}
-
-        def make_raw(h):
-            for nm in ("q", "pq"):
-                raw[(nm, h)] = keep.tile([P, NT, D], BF16, tag="raw_" + nm, name="raw_" + nm)
+        for h in range(H):
             for nm in ("k", "pk"):
-                raw[(nm, h)] = keep.tile([P, NT // 2, 2, D], BF16, tag="raw_" + nm, name="raw_" + nm)
-
+                raw[(nm, h)] = keep.tile([P, NT // 2, 2, D], BF16, name="raw_%s%d" % (nm, h))
+            for nm in ("q", "pq"):
+                raw[(nm, h)] = keep.tile([P, NT, D], BF16, name="raw_%s%d" % (nm, h))
         qq = [keep.tile([P, 2, NT, P], BF16, name="qq%d" % h) for h in range(H)]
         kk = [keep.tile([P, 2, 2, HALF], BF16, name="kk%d" % h) for h in range(H)]
         mb = [keep.tile([P, L], BF16, name="mb%d" % i) for i in range(NT)]
@@ -93,7 +92,6 @@ def tile_attention_kernel(tc, q, k, v, pe_q, pe_k, mask, out):
                 in_=v[0, h].rearrange("(g p t) n -> p g (t n)", p=P, t=4),
             )
 
-        make_raw(0)
         load_keys("k", k, 0, 0, 4)
         load_keys("pk", pe_k, 0, 0, 4)
         load_queries("q", q, 0, 0, 4)
@@ -102,10 +100,9 @@ def tile_attention_kernel(tc, q, k, v, pe_q, pe_k, mask, out):
         load_keys("k", k, 0, 4, 8)
         load_keys("pk", pe_k, 0, 4, 8)
         load_mask(1)
+        load_mask(2)
         load_queries("q", q, 0, 4, NT)
         load_queries("pq", pe_q, 0, 4, NT)
-        load_mask(2)
-        load_v(0)
 
         warm = small.tile([P, 1], F32, tag="warm", name="warm", bufs=1)
         nc.vector.memset(warm[:], 0.0)
@@ -136,9 +133,9 @@ def tile_attention_kernel(tc, q, k, v, pe_q, pe_k, mask, out):
                 in_=vg[h][:].rearrange("p g n u e -> p (g n u e)"),
             )
 
-        def flip_keys(h, j, copy):
+        def flip_keys(h, j, copy, pool, tag):
             u, a = divmod(j, 2)
-            bank = ps_s.tile([P, 2, 4, P], BF16, tag="s", name="flip")
+            bank = pool.tile([P, 2, 4, P], BF16, tag=tag, name="flip")
             for x, nm in enumerate(("k", "pk")):
                 for m in range(4):
                     nc.tensor.transpose(bank[:, x, m, :], raw[(nm, h)][:, 4 * a + m, u, :], ident[:])
@@ -147,20 +144,23 @@ def tile_attention_kernel(tc, q, k, v, pe_q, pe_k, mask, out):
                 in_=bank[:].rearrange("p x m r -> p x (m r)"),
             )
 
-        def flip_queries(h, c, copy):
-            bank = ps_s.tile([P, 2, 4, P], BF16, tag="s", name="flip")
+        def flip_queries(h, c, copy, pool, tag):
+            bank = pool.tile([P, 2, 4, P], BF16, tag=tag, name="flip")
             for x, nm in enumerate(("q", "pq")):
                 for t in range(4):
                     nc.tensor.transpose(bank[:, x, t, :], raw[(nm, h)][:, 4 * c + t, :], ident[:])
             dst = qq[h][:, :, 4 * c:4 * c + 4, :].rearrange("p x c r -> p x (c r)")
             copy(out=dst, in_=bank[:].rearrange("p x c r -> p x (c r)"))
 
+        vcopy = nc.vector.tensor_copy
+        scopy = nc.scalar.copy
+
         st = {}
 
         def role(u, j):
-            if j == NCH - 1 and u % 4 != 3:
+            if j == NCH - 1 and (u % 4 != 3 or u == NU - 1):
                 return "T"
-            if j == 0 and 3 <= u < NU - 2:
+            if j == 0 and FIRST_G <= u < NU - 2:
                 return "G"
             return "V"
 
@@ -168,9 +168,9 @@ def tile_attention_kernel(tc, q, k, v, pe_q, pe_k, mask, out):
             n0 = CH * (j % 2)
             return kk[h][:, x, j // 2, n0:n0 + CH]
 
-        def scores(u):
+        def scores(u, banks=ORDER):
             h, i = divmod(u, NT)
-            for j in ORDER:
+            for j in banks:
                 s = ps_s.tile([P, CH], F32, tag="s", name="s")
                 nc.tensor.matmul(s[:], lhsT=qq[h][:, 0, i, :], rhs=keys(h, 0, j), start=True, stop=False)
                 extra = role(u, j) == "T"
@@ -184,13 +184,11 @@ def tile_attention_kernel(tc, q, k, v, pe_q, pe_k, mask, out):
         def w_columns(u, j):
             return st[("w", u)][:, PAD + CH * j:PAD + CH * (j + 1)]
 
-        def leave_psum(u, who):
+        def leave_psum(u, banks):
             i = u % NT
             if ("w", u) not in st:
                 st[("w", u)] = wpool.tile([P, PAD + L], F32, tag="w", name="w")
-            for j in ORDER:
-                if role(u, j) not in who:
-                    continue
+            for j in banks:
                 s = st[("s", u, j)]
                 bias = mb[i][:, CH * j:CH * (j + 1)]
                 dst = w_columns(u, j)
@@ -216,19 +214,21 @@ def tile_attention_kernel(tc, q, k, v, pe_q, pe_k, mask, out):
 
         def exponent(u):
             e = epool.tile([P, L], BF16, tag="e", name="e")
-            rs = small.tile([P, 1], F32, tag="rs", name="rs")
+            if u % 2 == 0:
+                st[("rs", u // 2)] = small.tile([P, 2], F32, tag="rs", name="rs")
+            rs = st[("rs", u // 2)]
             nc.scalar.activation(
                 out=e[:], in_=st[("w", u)][:, PAD:PAD + L], func=ACT.Exp, bias=st[("wmin", u)][:], scale=-1.0,
-                accum_out=rs[:],
+                accum_out=rs[:, u % 2:u % 2 + 1],
             )
             st[("e", u)] = e
-            st[("rs", u)] = rs
 
         def flip_e(u):
             words = st[("e", u)][:].bitcast(F32)
             banks = []
             for b in range(2):
-                xt = ps_x.tile([P, 2, 2, P], F32, tag="xt", name="xt")
+                pool, tag = (ps_s, "s") if u >= NU - 2 else (ps_x, "xt")
+                xt = pool.tile([P, 2, 2, P], F32, tag=tag, name="xt")
                 for n in range(2):
                     g = 2 * b + n
                     for half in range(2):
@@ -237,16 +237,16 @@ def tile_attention_kernel(tc, q, k, v, pe_q, pe_k, mask, out):
                 banks.append(xt)
             st[("xt", u)] = banks
 
-        def group_e(u):
-            gr = gpool.tile([P, NCH, P, 4], BF16, tag="gr", name="gr", align_bytes=64)
-            grw = gr[:].rearrange("p g r t -> p (g r t)").bitcast(F32).rearrange("p (g r u) -> p g r u", r=P, u=2)
-            for b in range(2):
-                copy = nc.vector.tensor_copy if (u >= NU - 2 and b == 0) else nc.scalar.copy
+        def group_e(u, copies=None):
+            if ("gr", u) not in st:
+                st[("gr", u)] = gpool.tile([P, NCH, P, 4], BF16, tag="gr", name="gr", bufs=3, align_bytes=64)
+            flat = st[("gr", u)][:].rearrange("p g r t -> p (g r t)").bitcast(F32)
+            words = flat.rearrange("p (g r u) -> p g r u", r=P, u=2)
+            for b, copy in enumerate(copies or (scopy, scopy)):
                 copy(
-                    out=grw[:, 2 * b:2 * b + 2, :, :],
+                    out=words[:, 2 * b:2 * b + 2, :, :],
                     in_=st[("xt", u)][b][:].rearrange("p g u r -> p g r u"),
                 )
-            st[("gr", u)] = gr
 
         def quantise_e(u):
             codes = cpool.tile([P, NCH * P], U32, tag="codes", name="codes", align_bytes=64)
@@ -255,15 +255,18 @@ def tile_attention_kernel(tc, q, k, v, pe_q, pe_k, mask, out):
                 out=codes[:].bitcast(FP8X4), scales=scl[:],
                 in_=st[("gr", u)][:].rearrange("p g r t -> p (g r t)"),
             )
-            rinv = small.tile([P, 1], F32, tag="rinv", name="rinv")
-            nc.vector.reciprocal(rinv[:], st[("rs", u)][:])
             st[("codes", u)] = codes
             st[("scl", u)] = scl
-            st[("rinv", u)] = rinv
+
+        def invert_sums(n):
+            rinv = small.tile([P, 2], F32, tag="rinv", name="rinv")
+            nc.vector.reciprocal(rinv[:], st[("rs", n)][:])
+            st[("rinv", n)] = rinv
 
         def weighted_sum(u):
             h, i = divmod(u, NT)
-            o = ps_o.tile([P, DV], F32, tag="o", name="o")
+            pool, tag = (ps_s, "s") if u >= NU - 4 else (ps_o, "o")
+            o = pool.tile([P, DV], F32, tag=tag, name="o")
             for g in range(NCH):
                 nc.tensor.matmul_mx(
                     out=o[:],
@@ -279,77 +282,113 @@ def tile_attention_kernel(tc, q, k, v, pe_q, pe_k, mask, out):
             h, i = divmod(u, NT)
             o = st[("o", u)]
             res = opool.tile([P, DV], F32, tag="res", name="res")
-            nc.scalar.activation(out=res[:], in_=o[:], func=ACT.Copy, scale=st[("rinv", u)][:])
+            nc.scalar.activation(out=res[:], in_=o[:], func=ACT.Copy, scale=st[("rinv", u // 2)][:, u % 2:u % 2 + 1])
             nc.sync.dma_start(out=out[0, h].rearrange("(p t) n -> t p n", t=NT)[i], in_=res[:])
 
-        vcopy = nc.vector.tensor_copy
-        scopy = nc.scalar.copy
-        flip_keys(0, 0, vcopy)
-        flip_queries(0, 0, scopy)
-        flip_keys(0, 2, scopy)
+        flip_keys(0, 0, vcopy, ps_s, "s")
+        flip_queries(0, 0, scopy, ps_s, "s")
+        flip_keys(0, 2, scopy, ps_s, "s")
         for half in range(2):
             bias_from_mask(nc.vector, 0, CH * half, CH * (half + 1))
-        flip_keys(0, 1, vcopy)
-        flip_keys(0, 3, scopy)
-        bias_from_mask(nc.gpsimd, 1, 0, HALF)
-        bias_from_mask(nc.gpsimd, 2, 0, HALF)
-        load_mask(3)
+        flip_keys(0, 1, vcopy, ps_s, "s")
+        flip_keys(0, 3, scopy, ps_s, "s")
         scores(0)
-        for c in range(1, 4):
-            flip_queries(0, c, scopy)
-        make_raw(1)
+        load_mask(3)
         load_keys("k", k, 1, 0, 8)
         load_keys("pk", pe_k, 1, 0, 8)
+        for i in range(1, 5):
+            bias_from_mask(nc.gpsimd, i, 0, HALF)
+            if i == 1:
+                load_mask(4)
+                load_v(0)
+                load_queries("q", q, 1, 0, NT)
+                load_queries("pq", pe_q, 1, 0, NT)
 
-        later = {}
-        for c in range(4):
-            later[3 + c] = ("k", c)
-            later[7 + c] = ("q", c)
+        later = {
+            0: [("q", 0, 1)],
+            1: [("q", 0, 2), ("q", 0, 3)] + [("k", 1, c) for c in range(2)],
+            2: [("k", 1, c) for c in range(2, 4)] + [("q", 1, c) for c in range(4)],
+        }
+
+        def turn(s):
+            for kind, h, c in later.get(s, []):
+                if kind == "k":
+                    flip_keys(h, c, scopy, ps_x, "xt")
+                else:
+                    flip_queries(h, c, scopy, ps_x, "xt")
 
         with tc.manual_schedule():
-            for s in range(NU + 3):
-                if s < NU:
-                    leave_psum(s, "VTG")
-                if s >= 3 and s - 3 < NU:
-                    quantise_e(s - 3)
-                if s == 3:
+            for s in range(NU):
+                leave_psum(s, [j for j in ORDER if role(s, j) == "G"])
+                leave_psum(s, [j for j in ORDER if role(s, j) != "G"])
+                if s < FIRST_G:
+                    find_min(s)
+                elif s > FIRST_G:
+                    find_min(s - 1)
+                if s >= 4:
+                    quantise_e(s - 4)
+                    if s % 2 == 0:
+                        invert_sums((s - 4) // 2)
+                if s == 5:
                     quantise_v(0)
                 if s == 18:
                     quantise_v(1)
-                if s < NU:
-                    find_min(s)
-                if 2 <= s <= NU + 1:
-                    flip_e(s - 2)
+                if s == 0:
+                    turn(0)
                 if s + 1 < NU:
-                    scores(s + 1)
-                if s >= 4:
-                    finish(s - 4)
-                if 1 <= s <= NU:
+                    scores(s + 1, ORDER[:2])
+                if s >= 3:
+                    flip_e(s - 3)
+                if s + 1 < NU:
+                    scores(s + 1, ORDER[2:])
+                if s >= 5:
+                    weighted_sum(s - 5)
+                if s >= 6:
+                    finish(s - 6)
+                if 1 <= s <= FIRST_G:
                     exponent(s - 1)
-                if 2 <= s <= NU + 1:
-                    group_e(s - 2)
-                if s >= 3 and s - 3 < NU:
-                    weighted_sum(s - 3)
-                if s + 4 < NT:
+                elif s >= FIRST_G + 2:
+                    exponent(s - 2)
+                if s >= 3:
+                    group_e(s - 3)
+                if s > 0:
+                    turn(s)
+                if 1 <= s and s + 4 < NT:
                     load_mask(s + 4)
-                if s == 1:
-                    for g in range(NCH):
-                        regroup_v(0, g)
-                else:
-                    i = s + 3 if s == 0 else s + 2
-                    if i < NT:
-                        bias_from_mask(nc.gpsimd, i, 0, HALF)
-                if s == 1:
-                    load_queries("q", q, 1, 0, NT)
-                    load_queries("pq", pe_q, 1, 0, NT)
+                if s in (2, 4):
+                    regroup_v(0, s - 2)
+                    regroup_v(0, s - 1)
+                if 3 <= s and s + 2 < NT:
+                    bias_from_mask(nc.gpsimd, s + 2, 0, HALF)
                 if s == 3:
                     load_v(1)
                 if 14 <= s < 18:
                     regroup_v(1, s - 14)
-                if s in later:
-                    kind, c = later[s]
-                    if kind == "k":
-                        flip_keys(1, c, scopy)
-                    else:
-                        flip_queries(1, c, scopy)
-            finish(NU - 1)
+
+            x, y, z = NU - 3, NU - 2, NU - 1
+            find_min(z)
+            weighted_sum(NU - 5)
+            finish(NU - 6)
+            exponent(y)
+            flip_e(x)
+            quantise_e(NU - 4)
+            finish(NU - 5)
+            exponent(z)
+            invert_sums(NU // 2 - 2)
+            weighted_sum(NU - 4)
+            group_e(x, (vcopy, vcopy))
+            quantise_e(x)
+            flip_e(y)
+            weighted_sum(x)
+            group_e(y, (vcopy, vcopy))
+            finish(NU - 4)
+            finish(x)
+            quantise_e(y)
+            flip_e(z)
+            weighted_sum(y)
+            group_e(z, (vcopy, scopy))
+            quantise_e(z)
+            invert_sums(NU // 2 - 1)
+            finish(y)
+            weighted_sum(z)
+            finish(z)

@@ -40,7 +40,7 @@ def tile_attention_kernel(tc, q, k, v, pe_q, pe_k, mask, out):
         epool = ctx.enter_context(tc.tile_pool(name="epool", bufs=3))
         gpool = ctx.enter_context(tc.tile_pool(name="gpool", bufs=2))
         cpool = ctx.enter_context(tc.tile_pool(name="cpool", bufs=3))
-        opool = ctx.enter_context(tc.tile_pool(name="opool", bufs=3))
+        opool = ctx.enter_context(tc.tile_pool(name="opool", bufs=6))
         small = ctx.enter_context(tc.tile_pool(name="small", bufs=6))
         ps_s = ctx.enter_context(tc.psum_pool(name="ps_s", bufs=5))
         ps_x = ctx.enter_context(tc.psum_pool(name="ps_x", bufs=2))
@@ -158,11 +158,14 @@ def tile_attention_kernel(tc, q, k, v, pe_q, pe_k, mask, out):
         st = {}
 
         def role(u, j):
-            if j == NCH - 1 and (u % 4 != 3 or u == NU - 1):
+            if j == NCH - 1 and (u % 4 != 0 or u >= NU - 4):
                 return "T"
-            if j == 0 and FIRST_G <= u < NU - 2:
+            if j == 1 and u >= FIRST_G:
                 return "G"
             return "V"
+
+        def mask_of(u, j):
+            return mb[u % NT][:, CH * j:CH * (j + 1)]
 
         def keys(h, x, j):
             n0 = CH * (j % 2)
@@ -176,21 +179,17 @@ def tile_attention_kernel(tc, q, k, v, pe_q, pe_k, mask, out):
                 extra = role(u, j) == "T"
                 nc.tensor.matmul(s[:], lhsT=qq[h][:, 1, i, :], rhs=keys(h, 1, j), start=False, stop=not extra)
                 if extra:
-                    nc.tensor.matmul(
-                        s[:], lhsT=negident[:], rhs=mb[i][:, CH * j:CH * (j + 1)], start=False, stop=True
-                    )
+                    nc.tensor.matmul(s[:], lhsT=negident[:], rhs=mask_of(u, j), start=False, stop=True)
                 st[("s", u, j)] = s
 
         def w_columns(u, j):
             return st[("w", u)][:, PAD + CH * j:PAD + CH * (j + 1)]
 
         def leave_psum(u, banks):
-            i = u % NT
             if ("w", u) not in st:
                 st[("w", u)] = wpool.tile([P, PAD + L], F32, tag="w", name="w")
             for j in banks:
                 s = st[("s", u, j)]
-                bias = mb[i][:, CH * j:CH * (j + 1)]
                 dst = w_columns(u, j)
                 if role(u, j) == "T":
                     nc.vector.tensor_scalar(
@@ -199,10 +198,10 @@ def tile_attention_kernel(tc, q, k, v, pe_q, pe_k, mask, out):
                     )
                 elif role(u, j) == "G":
                     nc.scalar.activation(out=dst, in_=s[:], func=ACT.Copy, scale=-SCALE)
-                    nc.gpsimd.tensor_tensor(out=dst, in0=dst, in1=bias, op=ALU.add)
+                    nc.gpsimd.tensor_tensor(out=dst, in0=dst, in1=mask_of(u, j), op=ALU.add)
                 else:
                     nc.vector.scalar_tensor_tensor(
-                        out=dst, in0=s[:], scalar=-SCALE, in1=bias, op0=ALU.mult, op1=ALU.add,
+                        out=dst, in0=s[:], scalar=-SCALE, in1=mask_of(u, j), op0=ALU.mult, op1=ALU.add,
                     )
 
         def find_min(u):
@@ -212,21 +211,35 @@ def tile_attention_kernel(tc, q, k, v, pe_q, pe_k, mask, out):
             nc.vector.tensor_reduce(out=wmin[:], in_=st[("w", u)][:, cols], axis=AX.X, op=ALU.min)
             st[("wmin", u)] = wmin
 
+        def slot_of(u):
+            return (u // 4, u % 4) if u < NU - 1 else (NU // 4, 0)
+
         def exponent(u):
             e = epool.tile([P, L], BF16, tag="e", name="e")
-            if u % 2 == 0:
-                st[("rs", u // 2)] = small.tile([P, 2], F32, tag="rs", name="rs")
-            rs = st[("rs", u // 2)]
+            n, c = slot_of(u)
+            if c == 0:
+                st[("rs", n)] = small.tile([P, 4], F32, tag="rs", name="rs")
             nc.scalar.activation(
                 out=e[:], in_=st[("w", u)][:, PAD:PAD + L], func=ACT.Exp, bias=st[("wmin", u)][:], scale=-1.0,
-                accum_out=rs[:, u % 2:u % 2 + 1],
+                accum_out=st[("rs", n)][:, c:c + 1],
             )
             st[("e", u)] = e
 
-        def flip_e(u):
+        def exponent_half(u, b):
+            n = slot_of(u)[0]
+            if b == 0:
+                st[("e", u)] = epool.tile([P, L], BF16, tag="e", name="e")
+                st[("rs", n)] = small.tile([P, 4], F32, tag="rs", name="rs")
+            part = slice(CH * b, CH * (b + 1))
+            nc.scalar.activation(
+                out=st[("e", u)][:].rearrange("p (u n) -> p u n", u=2)[:, :, part],
+                in_=st[("w", u)][:, PAD:PAD + L].rearrange("p (u n) -> p u n", u=2)[:, :, part],
+                func=ACT.Exp, bias=st[("wmin", u)][:], scale=-1.0, accum_out=st[("rs", n)][:, b:b + 1],
+            )
+
+        def flip_e(u, halves=(0, 1)):
             words = st[("e", u)][:].bitcast(F32)
-            banks = []
-            for b in range(2):
+            for b in halves:
                 pool, tag = (ps_s, "s") if u >= NU - 2 else (ps_x, "xt")
                 xt = pool.tile([P, 2, 2, P], F32, tag=tag, name="xt")
                 for n in range(2):
@@ -234,38 +247,37 @@ def tile_attention_kernel(tc, q, k, v, pe_q, pe_k, mask, out):
                     for half in range(2):
                         lo = CH * half + P * g
                         nc.tensor.transpose(xt[:, n, half, :], words[:, lo:lo + P], ident32[:])
-                banks.append(xt)
-            st[("xt", u)] = banks
+                st[("xt", u, b)] = xt
 
-        def group_e(u, copies=None):
+        def group_half(u, b, copy):
             if ("gr", u) not in st:
                 st[("gr", u)] = gpool.tile([P, NCH, P, 4], BF16, tag="gr", name="gr", bufs=3, align_bytes=64)
             flat = st[("gr", u)][:].rearrange("p g r t -> p (g r t)").bitcast(F32)
             words = flat.rearrange("p (g r u) -> p g r u", r=P, u=2)
-            for b, copy in enumerate(copies or (scopy, scopy)):
-                copy(
-                    out=words[:, 2 * b:2 * b + 2, :, :],
-                    in_=st[("xt", u)][b][:].rearrange("p g u r -> p g r u"),
-                )
+            copy(out=words[:, 2 * b:2 * b + 2, :, :], in_=st[("xt", u, b)][:].rearrange("p g u r -> p g r u"))
 
-        def quantise_e(u):
-            codes = cpool.tile([P, NCH * P], U32, tag="codes", name="codes", align_bytes=64)
-            scl = cpool.tile([P, NCH * P], U8, tag="scl", name="scl", align_bytes=64)
+        def group_e(u, copies=None):
+            for b, copy in enumerate(copies or (scopy, scopy)):
+                group_half(u, b, copy)
+
+        def quantise_e(u, lo=0, hi=NCH):
+            if lo == 0:
+                st[("codes", u)] = cpool.tile([P, NCH * P], U32, tag="codes", name="codes", align_bytes=64)
+                st[("scl", u)] = cpool.tile([P, NCH * P], U8, tag="scl", name="scl", align_bytes=64)
             nc.vector.quantize_mx(
-                out=codes[:].bitcast(FP8X4), scales=scl[:],
-                in_=st[("gr", u)][:].rearrange("p g r t -> p (g r t)"),
+                out=st[("codes", u)][:, P * lo:P * hi].bitcast(FP8X4), scales=st[("scl", u)][:, P * lo:P * hi],
+                in_=st[("gr", u)][:, lo:hi, :, :].rearrange("p g r t -> p (g r t)"),
             )
-            st[("codes", u)] = codes
-            st[("scl", u)] = scl
 
         def invert_sums(n):
-            rinv = small.tile([P, 2], F32, tag="rinv", name="rinv")
-            nc.vector.reciprocal(rinv[:], st[("rs", n)][:])
+            rinv = small.tile([P, 4], F32, tag="rinv", name="rinv")
+            width = 4 if n < NU // 4 - 1 else 3 if n < NU // 4 else 1
+            nc.vector.reciprocal(rinv[:, :width], st[("rs", n)][:, :width])
             st[("rinv", n)] = rinv
 
         def weighted_sum(u):
             h, i = divmod(u, NT)
-            pool, tag = (ps_s, "s") if u >= NU - 4 else (ps_o, "o")
+            pool, tag = (ps_s, "s") if u >= NU - 6 else (ps_o, "o")
             o = pool.tile([P, DV], F32, tag=tag, name="o")
             for g in range(NCH):
                 nc.tensor.matmul_mx(
@@ -278,11 +290,17 @@ def tile_attention_kernel(tc, q, k, v, pe_q, pe_k, mask, out):
                 )
             st[("o", u)] = o
 
-        def finish(u):
+        def sscale(out, in_, factor):
+            nc.scalar.activation(out=out, in_=in_, func=ACT.Copy, scale=factor)
+
+        def vscale(out, in_, factor):
+            nc.vector.tensor_scalar(out=out, in0=in_, scalar1=factor, scalar2=None, op0=ALU.mult)
+
+        def finish(u, scaled=sscale):
             h, i = divmod(u, NT)
-            o = st[("o", u)]
+            n, c = slot_of(u)
             res = opool.tile([P, DV], F32, tag="res", name="res")
-            nc.scalar.activation(out=res[:], in_=o[:], func=ACT.Copy, scale=st[("rinv", u // 2)][:, u % 2:u % 2 + 1])
+            scaled(res[:], st[("o", u)][:], st[("rinv", n)][:, c:c + 1])
             nc.sync.dma_start(out=out[0, h].rearrange("(p t) n -> t p n", t=NT)[i], in_=res[:])
 
         flip_keys(0, 0, vcopy, ps_s, "s")
@@ -320,6 +338,8 @@ def tile_attention_kernel(tc, q, k, v, pe_q, pe_k, mask, out):
         with tc.manual_schedule():
             for s in range(NU):
                 leave_psum(s, [j for j in ORDER if role(s, j) == "G"])
+                if s % 4 == 2 and s >= 6:
+                    invert_sums((s - 6) // 4)
                 leave_psum(s, [j for j in ORDER if role(s, j) != "G"])
                 if s < FIRST_G:
                     find_min(s)
@@ -327,12 +347,14 @@ def tile_attention_kernel(tc, q, k, v, pe_q, pe_k, mask, out):
                     find_min(s - 1)
                 if s >= 4:
                     quantise_e(s - 4)
-                    if s % 2 == 0:
-                        invert_sums((s - 4) // 2)
                 if s == 5:
                     quantise_v(0)
                 if s == 18:
                     quantise_v(1)
+                if 1 <= s <= FIRST_G:
+                    exponent(s - 1)
+                elif s >= FIRST_G + 2:
+                    exponent(s - 2)
                 if s == 0:
                     turn(0)
                 if s + 1 < NU:
@@ -345,10 +367,6 @@ def tile_attention_kernel(tc, q, k, v, pe_q, pe_k, mask, out):
                     weighted_sum(s - 5)
                 if s >= 6:
                     finish(s - 6)
-                if 1 <= s <= FIRST_G:
-                    exponent(s - 1)
-                elif s >= FIRST_G + 2:
-                    exponent(s - 2)
                 if s >= 3:
                     group_e(s - 3)
                 if s > 0:
@@ -367,28 +385,34 @@ def tile_attention_kernel(tc, q, k, v, pe_q, pe_k, mask, out):
 
             x, y, z = NU - 3, NU - 2, NU - 1
             find_min(z)
-            weighted_sum(NU - 5)
-            finish(NU - 6)
             exponent(y)
             flip_e(x)
+            weighted_sum(NU - 5)
             quantise_e(NU - 4)
-            finish(NU - 5)
-            exponent(z)
-            invert_sums(NU // 2 - 2)
-            weighted_sum(NU - 4)
+            exponent_half(z, 0)
             group_e(x, (vcopy, vcopy))
+            finish(NU - 6, vscale)
             quantise_e(x)
+            finish(NU - 5, vscale)
             flip_e(y)
+            weighted_sum(NU - 4)
+            exponent_half(z, 1)
             weighted_sum(x)
+            invert_sums(NU // 4 - 1)
             group_e(y, (vcopy, vcopy))
-            finish(NU - 4)
-            finish(x)
+            flip_e(z, (0,))
+            group_half(z, 0, scopy)
             quantise_e(y)
-            flip_e(z)
+            finish(NU - 4)
+            flip_e(z, (1,))
             weighted_sum(y)
-            group_e(z, (vcopy, scopy))
-            quantise_e(z)
-            invert_sums(NU // 2 - 1)
+            finish(x)
+            quantise_e(z, 0, 2)
+            group_half(z, 1, vcopy)
+            rs = st[("rs", NU // 4)]
+            nc.vector.tensor_tensor(out=rs[:, 0:1], in0=rs[:, 0:1], in1=rs[:, 1:2], op=ALU.add)
+            quantise_e(z, 2, NCH)
+            invert_sums(NU // 4)
             finish(y)
             weighted_sum(z)
             finish(z)

@@ -92,10 +92,10 @@ def tile_attention_kernel(tc, q, k, v, pe_q, pe_k, mask, out):
                 in_=v[0, h].rearrange("(g p t) n -> p g (t n)", p=P, t=4),
             )
 
-        load_keys("k", k, 0, 0, 4)
-        load_keys("pk", pe_k, 0, 0, 4)
         load_queries("q", q, 0, 0, 4)
         load_queries("pq", pe_q, 0, 0, 4)
+        load_keys("k", k, 0, 0, 4)
+        load_keys("pk", pe_k, 0, 0, 4)
         load_mask(0)
         load_keys("k", k, 0, 4, 8)
         load_keys("pk", pe_k, 0, 4, 8)
@@ -144,13 +144,12 @@ def tile_attention_kernel(tc, q, k, v, pe_q, pe_k, mask, out):
                 in_=bank[:].rearrange("p x m r -> p x (m r)"),
             )
 
-        def flip_queries(h, c, copy, pool, tag):
+        def flip_queries(h, lo, hi, copy, pool, tag):
             bank = pool.tile([P, 2, 4, P], BF16, tag=tag, name="flip")
             for x, nm in enumerate(("q", "pq")):
-                for t in range(4):
-                    nc.tensor.transpose(bank[:, x, t, :], raw[(nm, h)][:, 4 * c + t, :], ident[:])
-            dst = qq[h][:, :, 4 * c:4 * c + 4, :].rearrange("p x c r -> p x (c r)")
-            copy(out=dst, in_=bank[:].rearrange("p x c r -> p x (c r)"))
+                for t in range(lo, hi):
+                    nc.tensor.transpose(bank[:, x, t - lo, :], raw[(nm, h)][:, t, :], ident[:])
+            copy(out=qq[h][:, :, lo:hi, :], in_=bank[:, :, :hi - lo, :])
 
         vcopy = nc.vector.tensor_copy
         scopy = nc.scalar.copy
@@ -303,25 +302,6 @@ def tile_attention_kernel(tc, q, k, v, pe_q, pe_k, mask, out):
             scaled(res[:], st[("o", u)][:], st[("rinv", n)][:, c:c + 1])
             nc.sync.dma_start(out=out[0, h].rearrange("(p t) n -> t p n", t=NT)[i], in_=res[:])
 
-        flip_keys(0, 0, vcopy, ps_s, "s")
-        flip_queries(0, 0, scopy, ps_s, "s")
-        flip_keys(0, 2, scopy, ps_s, "s")
-        for half in range(2):
-            bias_from_mask(nc.vector, 0, CH * half, CH * (half + 1))
-        flip_keys(0, 1, vcopy, ps_s, "s")
-        flip_keys(0, 3, scopy, ps_s, "s")
-        scores(0)
-        load_mask(3)
-        load_keys("k", k, 1, 0, 8)
-        load_keys("pk", pe_k, 1, 0, 8)
-        for i in range(1, 5):
-            bias_from_mask(nc.gpsimd, i, 0, HALF)
-            if i == 1:
-                load_mask(4)
-                load_v(0)
-                load_queries("q", q, 1, 0, NT)
-                load_queries("pq", pe_q, 1, 0, NT)
-
         later = {
             0: [("q", 0, 1)],
             1: [("q", 0, 2), ("q", 0, 3)] + [("k", 1, c) for c in range(2)],
@@ -333,14 +313,38 @@ def tile_attention_kernel(tc, q, k, v, pe_q, pe_k, mask, out):
                 if kind == "k":
                     flip_keys(h, c, scopy, ps_x, "xt")
                 else:
-                    flip_queries(h, c, scopy, ps_x, "xt")
+                    flip_queries(h, 4 * c, 4 * c + 4, scopy, ps_x, "xt")
 
         with tc.manual_schedule():
+            flip_queries(0, 0, 1, scopy, ps_x, "xt")
+            flip_keys(0, 0, vcopy, ps_s, "s")
+            flip_keys(0, 2, scopy, ps_s, "s")
+            for half in range(2):
+                bias_from_mask(nc.vector, 0, CH * half, CH * (half + 1))
+            scores(0, (0,))
+            flip_keys(0, 1, scopy, ps_s, "s")
+            scores(0, (2,))
+            flip_keys(0, 3, scopy, ps_x, "xt")
+            scores(0, (1,))
+            scores(0, (3,))
+            flip_queries(0, 1, 4, scopy, ps_x, "xt")
+            load_mask(3)
+            load_keys("k", k, 1, 0, 8)
+            load_keys("pk", pe_k, 1, 0, 8)
+            for i in range(1, 5):
+                bias_from_mask(nc.gpsimd, i, 0, HALF)
+                if i == 1:
+                    load_mask(4)
+                    load_v(0)
+                    load_queries("q", q, 1, 0, NT)
+                    load_queries("pq", pe_q, 1, 0, NT)
+
             for s in range(NU):
-                leave_psum(s, [j for j in ORDER if role(s, j) == "G"])
+                order = (0, 2, 1, 3) if s == 0 else ORDER
+                leave_psum(s, [j for j in order if role(s, j) == "G"])
                 if s % 4 == 2 and s >= 6:
                     invert_sums((s - 6) // 4)
-                leave_psum(s, [j for j in ORDER if role(s, j) != "G"])
+                leave_psum(s, [j for j in order if role(s, j) != "G"])
                 if s < FIRST_G:
                     find_min(s)
                 elif s > FIRST_G:

@@ -25,6 +25,13 @@ HALF = L // 2
 ORDER = (0, 1, 2, 3)
 SCALE = D ** -0.5
 BIG = 1.0e30
+REGS = {2: [0, 1], 3: [2], 4: [3]}
+NO_T = (0, 4, 8, 12, 16, 20, 24)
+NO_G = (7, 9, 11, 13)
+LATER = {0: [("q", 0, 1, "x")], 1: [("q", 0, 2, "x"), ("q", 0, 3, "x")], 4: [("k", 1, 0, "s")], 5: [("k", 1, 1, "s")], 6: [("k", 1, 2, "s")], 7: [("k", 1, 3, "s")], 9: [("q", 1, 0, "s")], 10: [("q", 1, 1, "s")], 11: [("q", 1, 2, "s")], 12: [("q", 1, 3, "s")]}
+LOADS = [("q", 0), ("m", 3), ("v", 0), ("m", 4)]
+SLOADS = dict([(1, [("m", 5), ("k", 1)]), (2, [("m", 6)]), (3, [("m", 7)]), (4, [("m", 8), ("q", 1)])] + [(s, [("m", s + 4)]) for s in range(5, 12)] + [(12, [("v", 1)])])
+REG0 = {}
 FIRST_G = 6
 PAD = 8
 
@@ -92,6 +99,18 @@ def tile_attention_kernel(tc, q, k, v, pe_q, pe_k, mask, out):
                 in_=v[0, h].rearrange("(g p t) n -> p g (t n)", p=P, t=4),
             )
 
+        def load(kind, n):
+            if kind == "m":
+                load_mask(n)
+            elif kind == "k":
+                load_keys("k", k, n, 0, 8)
+                load_keys("pk", pe_k, n, 0, 8)
+            elif kind == "v":
+                load_v(n)
+            else:
+                load_queries("q", q, n, 4 * (1 - n), NT)
+                load_queries("pq", pe_q, n, 4 * (1 - n), NT)
+
         load_queries("q", q, 0, 0, 4)
         load_queries("pq", pe_q, 0, 0, 4)
         load_keys("k", k, 0, 0, 4)
@@ -101,8 +120,6 @@ def tile_attention_kernel(tc, q, k, v, pe_q, pe_k, mask, out):
         load_keys("pk", pe_k, 0, 4, 8)
         load_mask(1)
         load_mask(2)
-        load_queries("q", q, 0, 4, NT)
-        load_queries("pq", pe_q, 0, 4, NT)
 
         warm = small.tile([P, 1], F32, tag="warm", name="warm", bufs=1)
         nc.vector.memset(warm[:], 0.0)
@@ -117,14 +134,15 @@ def tile_attention_kernel(tc, q, k, v, pe_q, pe_k, mask, out):
 
         vg = {}
 
-        def regroup_v(h, g):
+        def regroup_v(h, g, on_scalar=False):
             if g == 0:
                 vg[h] = gpool.tile([P, NCH, DV, 2, 2], BF16, tag="vg", name="vg", bufs=1, align_bytes=64)
-            nc.gpsimd.tensor_scalar(
-                out=vg[h][:, g, :, :, :],
-                in0=vraw[h][:, g, :, :].rearrange("p (e u) n -> p n u e", u=2),
-                scalar1=1.0, scalar2=0.0, op0=ALU.mult, op1=ALU.add,
-            )
+            dst = vg[h][:, g, :, :, :]
+            src = vraw[h][:, g, :, :].rearrange("p (e u) n -> p n u e", u=2)
+            if on_scalar:
+                nc.scalar.copy(out=dst, in_=src)
+            else:
+                nc.gpsimd.tensor_scalar(out=dst, in0=src, scalar1=1.0, scalar2=0.0, op0=ALU.mult, op1=ALU.add)
 
         def quantise_v(h):
             nc.vector.quantize_mx(
@@ -139,17 +157,21 @@ def tile_attention_kernel(tc, q, k, v, pe_q, pe_k, mask, out):
             for x, nm in enumerate(("k", "pk")):
                 for m in range(4):
                     nc.tensor.transpose(bank[:, x, m, :], raw[(nm, h)][:, 4 * a + m, u, :], ident[:])
-            copy(
-                out=kk[h][:, :, u, CH * a:CH * (a + 1)],
-                in_=bank[:].rearrange("p x m r -> p x (m r)"),
-            )
+            pending.append((copy, kk[h][:, :, u, CH * a:CH * (a + 1)], bank[:].rearrange("p x m r -> p x (m r)")))
 
         def flip_queries(h, lo, hi, copy, pool, tag):
             bank = pool.tile([P, 2, 4, P], BF16, tag=tag, name="flip")
             for x, nm in enumerate(("q", "pq")):
                 for t in range(lo, hi):
                     nc.tensor.transpose(bank[:, x, t - lo, :], raw[(nm, h)][:, t, :], ident[:])
-            copy(out=qq[h][:, :, lo:hi, :], in_=bank[:, :, :hi - lo, :])
+            pending.append((copy, qq[h][:, :, lo:hi, :], bank[:, :, :hi - lo, :]))
+
+        pending = []
+
+        def fetch():
+            while pending:
+                copy, out_, in_ = pending.pop(0)
+                copy(out=out_, in_=in_)
 
         vcopy = nc.vector.tensor_copy
         scopy = nc.scalar.copy
@@ -157,9 +179,9 @@ def tile_attention_kernel(tc, q, k, v, pe_q, pe_k, mask, out):
         st = {}
 
         def role(u, j):
-            if j == NCH - 1 and (u % 4 != 0 or u >= NU - 4):
+            if j == NCH - 1 and u not in NO_T:
                 return "T"
-            if j == 1 and u >= FIRST_G:
+            if j == 1 and u >= FIRST_G and u not in NO_G:
                 return "G"
             return "V"
 
@@ -239,7 +261,7 @@ def tile_attention_kernel(tc, q, k, v, pe_q, pe_k, mask, out):
         def flip_e(u, halves=(0, 1)):
             words = st[("e", u)][:].bitcast(F32)
             for b in halves:
-                pool, tag = (ps_s, "s") if u >= NU - 2 else (ps_x, "xt")
+                pool, tag = (ps_s, "s") if u >= NU - 3 and u != NU - 2 else (ps_x, "xt")
                 xt = pool.tile([P, 2, 2, P], F32, tag=tag, name="xt")
                 for n in range(2):
                     g = 2 * b + n
@@ -276,7 +298,7 @@ def tile_attention_kernel(tc, q, k, v, pe_q, pe_k, mask, out):
 
         def weighted_sum(u):
             h, i = divmod(u, NT)
-            pool, tag = (ps_s, "s") if u >= NU - 6 else (ps_o, "o")
+            pool, tag = (ps_s, "s") if u >= NU - 6 and u % 2 == 0 else (ps_o, "o")
             o = pool.tile([P, DV], F32, tag=tag, name="o")
             for g in range(NCH):
                 nc.tensor.matmul_mx(
@@ -302,42 +324,39 @@ def tile_attention_kernel(tc, q, k, v, pe_q, pe_k, mask, out):
             scaled(res[:], st[("o", u)][:], st[("rinv", n)][:, c:c + 1])
             nc.sync.dma_start(out=out[0, h].rearrange("(p t) n -> t p n", t=NT)[i], in_=res[:])
 
-        later = {
-            0: [("q", 0, 1)],
-            1: [("q", 0, 2), ("q", 0, 3)] + [("k", 1, c) for c in range(2)],
-            2: [("k", 1, c) for c in range(2, 4)] + [("q", 1, c) for c in range(4)],
-        }
+        later = LATER
 
         def turn(s):
-            for kind, h, c in later.get(s, []):
+            for kind, h, c, b in later.get(s, []):
+                pool, tag = {"x": (ps_x, "xt"), "s": (ps_s, "s"), "o": (ps_o, "o")}[b]
                 if kind == "k":
-                    flip_keys(h, c, scopy, ps_x, "xt")
+                    flip_keys(h, c, scopy, pool, tag)
                 else:
-                    flip_queries(h, 4 * c, 4 * c + 4, scopy, ps_x, "xt")
+                    flip_queries(h, 4 * c, 4 * c + 4, scopy, pool, tag)
 
         with tc.manual_schedule():
             flip_queries(0, 0, 1, scopy, ps_x, "xt")
+            fetch()
             flip_keys(0, 0, vcopy, ps_s, "s")
+            fetch()
             flip_keys(0, 2, scopy, ps_s, "s")
+            fetch()
             for half in range(2):
                 bias_from_mask(nc.vector, 0, CH * half, CH * (half + 1))
             scores(0, (0,))
             flip_keys(0, 1, scopy, ps_s, "s")
+            fetch()
             scores(0, (2,))
             flip_keys(0, 3, scopy, ps_x, "xt")
+            fetch()
             scores(0, (1,))
             scores(0, (3,))
             flip_queries(0, 1, 4, scopy, ps_x, "xt")
-            load_mask(3)
-            load_keys("k", k, 1, 0, 8)
-            load_keys("pk", pe_k, 1, 0, 8)
+            fetch()
+            for what in LOADS:
+                load(*what)
             for i in range(1, 5):
                 bias_from_mask(nc.gpsimd, i, 0, HALF)
-                if i == 1:
-                    load_mask(4)
-                    load_v(0)
-                    load_queries("q", q, 1, 0, NT)
-                    load_queries("pq", pe_q, 1, 0, NT)
 
             for s in range(NU):
                 order = (0, 2, 1, 3) if s == 0 else ORDER
@@ -359,31 +378,28 @@ def tile_attention_kernel(tc, q, k, v, pe_q, pe_k, mask, out):
                     exponent(s - 1)
                 elif s >= FIRST_G + 2:
                     exponent(s - 2)
-                if s == 0:
-                    turn(0)
+                fetch()
+                for g in REGS.get(s, []):
+                    regroup_v(0, g, True)
                 if s + 1 < NU:
                     scores(s + 1, ORDER[:2])
                 if s >= 3:
                     flip_e(s - 3)
                 if s + 1 < NU:
                     scores(s + 1, ORDER[2:])
+                turn(s)
                 if s >= 5:
                     weighted_sum(s - 5)
                 if s >= 6:
                     finish(s - 6)
                 if s >= 3:
                     group_e(s - 3)
-                if s > 0:
-                    turn(s)
-                if 1 <= s and s + 4 < NT:
-                    load_mask(s + 4)
-                if s in (2, 4):
-                    regroup_v(0, s - 2)
-                    regroup_v(0, s - 1)
+                for what in SLOADS.get(s, []):
+                    load(*what)
+                for g in REG0.get(s, []):
+                    regroup_v(0, g)
                 if 3 <= s and s + 2 < NT:
                     bias_from_mask(nc.gpsimd, s + 2, 0, HALF)
-                if s == 3:
-                    load_v(1)
                 if 14 <= s < 18:
                     regroup_v(1, s - 14)
 
@@ -394,25 +410,25 @@ def tile_attention_kernel(tc, q, k, v, pe_q, pe_k, mask, out):
             weighted_sum(NU - 5)
             quantise_e(NU - 4)
             exponent_half(z, 0)
+            weighted_sum(NU - 4)
             group_e(x, (vcopy, vcopy))
             finish(NU - 6, vscale)
             quantise_e(x)
             finish(NU - 5, vscale)
             flip_e(y)
-            weighted_sum(NU - 4)
             exponent_half(z, 1)
-            weighted_sum(x)
             invert_sums(NU // 4 - 1)
-            group_e(y, (vcopy, vcopy))
             flip_e(z, (0,))
-            group_half(z, 0, scopy)
-            quantise_e(y)
+            weighted_sum(x)
+            group_e(y, (vcopy, vcopy))
             finish(NU - 4)
             flip_e(z, (1,))
+            group_half(z, 0, scopy)
+            quantise_e(y)
             weighted_sum(y)
+            group_half(z, 1, vcopy)
             finish(x)
             quantise_e(z, 0, 2)
-            group_half(z, 1, vcopy)
             rs = st[("rs", NU // 4)]
             nc.vector.tensor_tensor(out=rs[:, 0:1], in0=rs[:, 0:1], in1=rs[:, 1:2], op=ALU.add)
             quantise_e(z, 2, NCH)

from contextlib import ExitStack

import concourse.mybir as mybir
from concourse.masks import make_identity

F32 = mybir.dt.float32
BF16 = mybir.dt.bfloat16
U32 = mybir.dt.uint32
U8 = mybir.dt.uint8
FP8X4 = mybir.dt.float8_e4m3fn_x4
ALU = mybir.AluOpType
ACT = mybir.ActivationFunctionType
AX = mybir.AxisListType

P = 128
H = 2
L = 2048
D = 128
DV = 256
NT = L // P
NU = H * NT
CH = 512
NCH = L // CH
HALF = L // 2
ORDER = (0, 1, 2, 3)
SCALE = D ** -0.5
BIG = 1.0e30
REGS = {2: [0, 1], 3: [2], 4: [3]}
NO_T = (0, 4, 8, 12, 16, 20, 24)
NO_G = (7, 9, 11, 13)
LATER = {0: [("q", 0, 1, "x")], 1: [("q", 0, 2, "x"), ("q", 0, 3, "x")], 4: [("k", 1, 0, "s")], 5: [("k", 1, 1, "s")], 6: [("k", 1, 2, "s")], 7: [("k", 1, 3, "s")], 9: [("q", 1, 0, "s")], 10: [("q", 1, 1, "s")], 11: [("q", 1, 2, "s")], 12: [("q", 1, 3, "s")]}
LOADS = [("q", 0), ("m", 3), ("v", 0), ("m", 4)]
SLOADS = dict([(1, [("m", 5), ("k", 1)]), (2, [("m", 6)]), (3, [("m", 7)]), (4, [("m", 8), ("q", 1)])] + [(s, [("m", s + 4)]) for s in range(5, 12)] + [(12, [("v", 1)])])
REG0 = {}
FIRST_G = 6
PAD = 8

FLOPS = 2 * H * L * L * (2 * D + DV)


def tile_attention_kernel(tc, q, k, v, pe_q, pe_k, mask, out):
    nc = tc.nc
    with ExitStack() as ctx:
        keep = ctx.enter_context(tc.tile_pool(name="keep", bufs=1))
        mpool = ctx.enter_context(tc.tile_pool(name="mpool", bufs=3))
        wpool = ctx.enter_context(tc.tile_pool(name="wpool", bufs=4))
        epool = ctx.enter_context(tc.tile_pool(name="epool", bufs=3))
        gpool = ctx.enter_context(tc.tile_pool(name="gpool", bufs=2))
        cpool = ctx.enter_context(tc.tile_pool(name="cpool", bufs=3))
        opool = ctx.enter_context(tc.tile_pool(name="opool", bufs=6))
        small = ctx.enter_context(tc.tile_pool(name="small", bufs=6))
        ps_s = ctx.enter_context(tc.psum_pool(name="ps_s", bufs=5))
        ps_x = ctx.enter_context(tc.psum_pool(name="ps_x", bufs=2))
        ps_o = ctx.enter_context(tc.psum_pool(name="ps_o", bufs=1))

        ident = keep.tile([P, P], BF16, name="ident")
        make_identity(nc, ident[:])
        ident32 = keep.tile([P, P], F32, name="ident32")
        make_identity(nc, ident32[:])
        negident = keep.tile([P, P], BF16, name="negident")
        nc.vector.tensor_scalar_mul(out=negident[:], in0=ident[:], scalar1=-1.0)

        raw = {}
        for h in range(H):
            for nm in ("k", "pk"):
                raw[(nm, h)] = keep.tile([P, NT // 2, 2, D], BF16, name="raw_%s%d" % (nm, h))
            for nm in ("q", "pq"):
                raw[(nm, h)] = keep.tile([P, NT, D], BF16, name="raw_%s%d" % (nm, h))
        qq = [keep.tile([P, 2, NT, P], BF16, name="qq%d" % h) for h in range(H)]
        kk = [keep.tile([P, 2, 2, HALF], BF16, name="kk%d" % h) for h in range(H)]
        mb = [keep.tile([P, L], BF16, name="mb%d" % i) for i in range(NT)]
        vcodes = [keep.tile([P, NCH * DV], U32, name="vcodes%d" % h, align_bytes=64) for h in range(H)]
        vscl = [keep.tile([P, NCH * DV], U8, name="vscl%d" % h, align_bytes=64) for h in range(H)]

        def load_keys(nm, src, h, lo, hi):
            nc.sync.dma_start(
                out=raw[(nm, h)][:, lo:hi, :, :].rearrange("p m u d -> p m (u d)"),
                in_=src[0, h].rearrange("(m p u) d -> p m (u d)", p=P, u=2)[:, lo:hi, :],
            )

        def load_queries(nm, src, h, lo, hi):
            nc.sync.dma_start(
                out=raw[(nm, h)][:, lo:hi, :],
                in_=src[0, h].rearrange("(p t) d -> p t d", t=NT)[:, lo:hi, :],
            )

        mraw = {}

        def load_mask(i):
            mraw[i] = mpool.tile([P, L], BF16, tag="mraw", name="mraw")
            nc.sync.dma_start(out=mraw[i][:], in_=mask[0].rearrange("(p t) c -> t p c", t=NT)[i])

        vraw = {}

        def load_v(h):
            vraw[h] = gpool.tile([P, NCH, 4, DV], BF16, tag="vraw", name="vraw", bufs=1)
            nc.sync.dma_start(
                out=vraw[h][:].rearrange("p g t n -> p g (t n)"),
                in_=v[0, h].rearrange("(g p t) n -> p g (t n)", p=P, t=4),
            )

        def load(kind, n):
            if kind == "m":
                load_mask(n)
            elif kind == "k":
                load_keys("k", k, n, 0, 8)
                load_keys("pk", pe_k, n, 0, 8)
            elif kind == "v":
                load_v(n)
            else:
                load_queries("q", q, n, 4 * (1 - n), NT)
                load_queries("pq", pe_q, n, 4 * (1 - n), NT)

        load_queries("q", q, 0, 0, 4)
        load_queries("pq", pe_q, 0, 0, 4)
        load_keys("k", k, 0, 0, 4)
        load_keys("pk", pe_k, 0, 0, 4)
        load_mask(0)
        load_keys("k", k, 0, 4, 8)
        load_keys("pk", pe_k, 0, 4, 8)
        load_mask(1)
        load_mask(2)

        warm = small.tile([P, 1], F32, tag="warm", name="warm", bufs=1)
        nc.vector.memset(warm[:], 0.0)
        nc.scalar.activation(out=warm[:], in_=warm[:], func=ACT.Exp)

        def bias_from_mask(eng, i, lo, hi):
            eng.tensor_scalar(
                out=mb[i][:].rearrange("p (u n) -> p u n", u=2)[:, :, lo:hi],
                in0=mraw[i][:].rearrange("p (n u) -> p u n", u=2)[:, :, lo:hi],
                scalar1=-1.0, scalar2=-BIG, op0=ALU.add, op1=ALU.mult,
            )

        vg = {}

        def regroup_v(h, g, on_scalar=False):
            if g == 0:
                vg[h] = gpool.tile([P, NCH, DV, 2, 2], BF16, tag="vg", name="vg", bufs=1, align_bytes=64)
            dst = vg[h][:, g, :, :, :]
            src = vraw[h][:, g, :, :].rearrange("p (e u) n -> p n u e", u=2)
            if on_scalar:
                nc.scalar.copy(out=dst, in_=src)
            else:
                nc.gpsimd.tensor_scalar(out=dst, in0=src, scalar1=1.0, scalar2=0.0, op0=ALU.mult, op1=ALU.add)

        def quantise_v(h):
            nc.vector.quantize_mx(
                out=vcodes[h][:].bitcast(FP8X4),
                scales=vscl[h][:],
                in_=vg[h][:].rearrange("p g n u e -> p (g n u e)"),
            )

        def flip_keys(h, j, copy, pool, tag):
            u, a = divmod(j, 2)
            bank = pool.tile([P, 2, 4, P], BF16, tag=tag, name="flip")
            for x, nm in enumerate(("k", "pk")):
                for m in range(4):
                    nc.tensor.transpose(bank[:, x, m, :], raw[(nm, h)][:, 4 * a + m, u, :], ident[:])
            pending.append((copy, kk[h][:, :, u, CH * a:CH * (a + 1)], bank[:].rearrange("p x m r -> p x (m r)")))

        def flip_queries(h, lo, hi, copy, pool, tag):
            bank = pool.tile([P, 2, 4, P], BF16, tag=tag, name="flip")
            for x, nm in enumerate(("q", "pq")):
                for t in range(lo, hi):
                    nc.tensor.transpose(bank[:, x, t - lo, :], raw[(nm, h)][:, t, :], ident[:])
            pending.append((copy, qq[h][:, :, lo:hi, :], bank[:, :, :hi - lo, :]))

        pending = []

        def fetch():
            while pending:
                copy, out_, in_ = pending.pop(0)
                copy(out=out_, in_=in_)

        vcopy = nc.vector.tensor_copy
        scopy = nc.scalar.copy

        st = {}

        def role(u, j):
            if j == NCH - 1 and u not in NO_T:
                return "T"
            if j == 1 and u >= FIRST_G and u not in NO_G:
                return "G"
            return "V"

        def mask_of(u, j):
            return mb[u % NT][:, CH * j:CH * (j + 1)]

        def keys(h, x, j):
            n0 = CH * (j % 2)
            return kk[h][:, x, j // 2, n0:n0 + CH]

        def scores(u, banks=ORDER):
            h, i = divmod(u, NT)
            for j in banks:
                s = ps_s.tile([P, CH], F32, tag="s", name="s")
                nc.tensor.matmul(s[:], lhsT=qq[h][:, 0, i, :], rhs=keys(h, 0, j), start=True, stop=False)
                extra = role(u, j) == "T"
                nc.tensor.matmul(s[:], lhsT=qq[h][:, 1, i, :], rhs=keys(h, 1, j), start=False, stop=not extra)
                if extra:
                    nc.tensor.matmul(s[:], lhsT=negident[:], rhs=mask_of(u, j), start=False, stop=True)
                st[("s", u, j)] = s

        def w_columns(u, j):
            return st[("w", u)][:, PAD + CH * j:PAD + CH * (j + 1)]

        def leave_psum(u, banks):
            if ("w", u) not in st:
                st[("w", u)] = wpool.tile([P, PAD + L], F32, tag="w", name="w")
            for j in banks:
                s = st[("s", u, j)]
                dst = w_columns(u, j)
                if role(u, j) == "T":
                    nc.vector.tensor_scalar(
                        out=dst, in0=s[:], scalar1=-SCALE, scalar2=None,
                        op0=ALU.mult, op1=ALU.min, accum_out=st[("w", u)][:, PAD - 1:PAD],
                    )
                elif role(u, j) == "G":
                    nc.scalar.activation(out=dst, in_=s[:], func=ACT.Copy, scale=-SCALE)
                    nc.gpsimd.tensor_tensor(out=dst, in0=dst, in1=mask_of(u, j), op=ALU.add)
                else:
                    nc.vector.scalar_tensor_tensor(
                        out=dst, in0=s[:], scalar=-SCALE, in1=mask_of(u, j), op0=ALU.mult, op1=ALU.add,
                    )

        def find_min(u):
            last = role(u, NCH - 1) == "T"
            cols = slice(PAD - 1, PAD + CH * (NCH - 1)) if last else slice(PAD, PAD + L)
            wmin = small.tile([P, 1], F32, tag="wmin", name="wmin")
            nc.vector.tensor_reduce(out=wmin[:], in_=st[("w", u)][:, cols], axis=AX.X, op=ALU.min)
            st[("wmin", u)] = wmin

        def slot_of(u):
            return (u // 4, u % 4) if u < NU - 1 else (NU // 4, 0)

        def exponent(u):
            e = epool.tile([P, L], BF16, tag="e", name="e")
            n, c = slot_of(u)
            if c == 0:
                st[("rs", n)] = small.tile([P, 4], F32, tag="rs", name="rs")
            nc.scalar.activation(
                out=e[:], in_=st[("w", u)][:, PAD:PAD + L], func=ACT.Exp, bias=st[("wmin", u)][:], scale=-1.0,
                accum_out=st[("rs", n)][:, c:c + 1],
            )
            st[("e", u)] = e

        def exponent_half(u, b):
            n = slot_of(u)[0]
            if b == 0:
                st[("e", u)] = epool.tile([P, L], BF16, tag="e", name="e")
                st[("rs", n)] = small.tile([P, 4], F32, tag="rs", name="rs")
            part = slice(CH * b, CH * (b + 1))
            nc.scalar.activation(
                out=st[("e", u)][:].rearrange("p (u n) -> p u n", u=2)[:, :, part],
                in_=st[("w", u)][:, PAD:PAD + L].rearrange("p (u n) -> p u n", u=2)[:, :, part],
                func=ACT.Exp, bias=st[("wmin", u)][:], scale=-1.0, accum_out=st[("rs", n)][:, b:b + 1],
            )

        def flip_e(u, halves=(0, 1)):
            words = st[("e", u)][:].bitcast(F32)
            for b in halves:
                pool, tag = (ps_s, "s") if u >= NU - 3 and u != NU - 2 else (ps_x, "xt")
                xt = pool.tile([P, 2, 2, P], F32, tag=tag, name="xt")
                for n in range(2):
                    g = 2 * b + n
                    for half in range(2):
                        lo = CH * half + P * g
                        nc.tensor.transpose(xt[:, n, half, :], words[:, lo:lo + P], ident32[:])
                st[("xt", u, b)] = xt

        def group_half(u, b, copy):
            if ("gr", u) not in st:
                st[("gr", u)] = gpool.tile([P, NCH, P, 4], BF16, tag="gr", name="gr", bufs=3, align_bytes=64)
            flat = st[("gr", u)][:].rearrange("p g r t -> p (g r t)").bitcast(F32)
            words = flat.rearrange("p (g r u) -> p g r u", r=P, u=2)
            copy(out=words[:, 2 * b:2 * b + 2, :, :], in_=st[("xt", u, b)][:].rearrange("p g u r -> p g r u"))

        def group_e(u, copies=None):
            for b, copy in enumerate(copies or (scopy, scopy)):
                group_half(u, b, copy)

        def quantise_e(u, lo=0, hi=NCH):
            if lo == 0:
                st[("codes", u)] = cpool.tile([P, NCH * P], U32, tag="codes", name="codes", align_bytes=64)
                st[("scl", u)] = cpool.tile([P, NCH * P], U8, tag="scl", name="scl", align_bytes=64)
            nc.vector.quantize_mx(
                out=st[("codes", u)][:, P * lo:P * hi].bitcast(FP8X4), scales=st[("scl", u)][:, P * lo:P * hi],
                in_=st[("gr", u)][:, lo:hi, :, :].rearrange("p g r t -> p (g r t)"),
            )

        def invert_sums(n):
            rinv = small.tile([P, 4], F32, tag="rinv", name="rinv")
            width = 4 if n < NU // 4 - 1 else 3 if n < NU // 4 else 1
            nc.vector.reciprocal(rinv[:, :width], st[("rs", n)][:, :width])
            st[("rinv", n)] = rinv

        def weighted_sum(u):
            h, i = divmod(u, NT)
            pool, tag = (ps_s, "s") if u >= NU - 6 and u % 2 == 0 else (ps_o, "o")
            o = pool.tile([P, DV], F32, tag=tag, name="o")
            for g in range(NCH):
                nc.tensor.matmul_mx(
                    out=o[:],
                    lhsT=st[("codes", u)][:, P * g:P * (g + 1)].bitcast(FP8X4),
                    lhsT_scale=st[("scl", u)][:, P * g:P * (g + 1)],
                    rhs=vcodes[h][:, DV * g:DV * (g + 1)].bitcast(FP8X4),
                    rhs_scale=vscl[h][:, DV * g:DV * (g + 1)],
                    start=(g == 0), stop=(g == NCH - 1),
                )
            st[("o", u)] = o

        def sscale(out, in_, factor):
            nc.scalar.activation(out=out, in_=in_, func=ACT.Copy, scale=factor)

        def vscale(out, in_, factor):
            nc.vector.tensor_scalar(out=out, in0=in_, scalar1=factor, scalar2=None, op0=ALU.mult)

        def finish(u, scaled=sscale):
            h, i = divmod(u, NT)
            n, c = slot_of(u)
            res = opool.tile([P, DV], F32, tag="res", name="res")
            scaled(res[:], st[("o", u)][:], st[("rinv", n)][:, c:c + 1])
            nc.sync.dma_start(out=out[0, h].rearrange("(p t) n -> t p n", t=NT)[i], in_=res[:])

        later = LATER

        def turn(s):
            for kind, h, c, b in later.get(s, []):
                pool, tag = {"x": (ps_x, "xt"), "s": (ps_s, "s"), "o": (ps_o, "o")}[b]
                if kind == "k":
                    flip_keys(h, c, scopy, pool, tag)
                else:
                    flip_queries(h, 4 * c, 4 * c + 4, scopy, pool, tag)

        with tc.manual_schedule():
            flip_queries(0, 0, 1, scopy, ps_x, "xt")
            fetch()
            flip_keys(0, 0, vcopy, ps_s, "s")
            fetch()
            flip_keys(0, 2, scopy, ps_s, "s")
            fetch()
            for half in range(2):
                bias_from_mask(nc.vector, 0, CH * half, CH * (half + 1))
            scores(0, (0,))
            flip_keys(0, 1, scopy, ps_s, "s")
            fetch()
            scores(0, (2,))
            flip_keys(0, 3, scopy, ps_x, "xt")
            fetch()
            scores(0, (1,))
            scores(0, (3,))
            flip_queries(0, 1, 4, scopy, ps_x, "xt")
            fetch()
            for what in LOADS:
                load(*what)
            for i in range(1, 5):
                bias_from_mask(nc.gpsimd, i, 0, HALF)

            for s in range(NU):
                order = (0, 2, 1, 3) if s == 0 else ORDER
                leave_psum(s, [j for j in order if role(s, j) == "G"])
                if s % 4 == 2 and s >= 6:
                    invert_sums((s - 6) // 4)
                leave_psum(s, [j for j in order if role(s, j) != "G"])
                if s < FIRST_G:
                    find_min(s)
                elif s > FIRST_G:
                    find_min(s - 1)
                if s >= 4:
                    quantise_e(s - 4)
                if s == 5:
                    quantise_v(0)
                if s == 18:
                    quantise_v(1)
                if 1 <= s <= FIRST_G:
                    exponent(s - 1)
                elif s >= FIRST_G + 2:
                    exponent(s - 2)
                fetch()
                for g in REGS.get(s, []):
                    regroup_v(0, g, True)
                if s + 1 < NU:
                    scores(s + 1, ORDER[:2])
                if s >= 3:
                    flip_e(s - 3)
                if s + 1 < NU:
                    scores(s + 1, ORDER[2:])
                turn(s)
                if s >= 5:
                    weighted_sum(s - 5)
                if s >= 6:
                    finish(s - 6)
                if s >= 3:
                    group_e(s - 3)
                for what in SLOADS.get(s, []):
                    load(*what)
                for g in REG0.get(s, []):
                    regroup_v(0, g)
                if 3 <= s and s + 2 < NT:
                    bias_from_mask(nc.gpsimd, s + 2, 0, HALF)
                if 14 <= s < 18:
                    regroup_v(1, s - 14)

            x, y, z = NU - 3, NU - 2, NU - 1
            find_min(z)
            exponent(y)
            flip_e(x)
            weighted_sum(NU - 5)
            quantise_e(NU - 4)
            exponent_half(z, 0)
            weighted_sum(NU - 4)
            group_e(x, (vcopy, vcopy))
            finish(NU - 6, vscale)
            quantise_e(x)
            finish(NU - 5, vscale)
            flip_e(y)
            exponent_half(z, 1)
            invert_sums(NU // 4 - 1)
            flip_e(z, (0,))
            weighted_sum(x)
            group_e(y, (vcopy, vcopy))
            finish(NU - 4)
            flip_e(z, (1,))
            group_half(z, 0, scopy)
            quantise_e(y)
            weighted_sum(y)
            group_half(z, 1, vcopy)
            finish(x)
            quantise_e(z, 0, 2)
            rs = st[("rs", NU // 4)]
            nc.vector.tensor_tensor(out=rs[:, 0:1], in0=rs[:, 0:1], in1=rs[:, 1:2], op=ALU.add)
            quantise_e(z, 2, NCH)
            invert_sums(NU // 4)
            finish(y)
            weighted_sum(z)
            finish(z)
